import numpy as np
import ml_dtypes

BF16 = ml_dtypes.bfloat16


def bf(x):
    return np.asarray(x, np.float32).astype(BF16)


def f32(x):
    return np.asarray(x, np.float32)


def f64(x):
    return np.asarray(x).astype(np.float64)


def striped(idx):
    return np.tile(idx.reshape(-1, 16).T, (8, 1))


F, H, D, R, M, C, N, S = 512, 4, 128, 2, 512, 1024, 1024, 2048
SLOPE = 0.2
DENSITY = 1.0 / 32.0
GAIN = 2.0


def setup_inputs():
    x = bf(np.random.standard_normal((F, N)))
    w = bf(GAIN * np.random.standard_normal((F, M)) / np.sqrt(F))
    att_self = bf(np.random.standard_normal((M, 1)) / (GAIN * np.sqrt(D)))
    att_neigh = bf(np.random.standard_normal((M, 1)) / (GAIN * np.sqrt(D)))
    b = f32(0.1 * np.random.standard_normal((M, 1)))
    adj_t = bf(np.maximum(np.random.random_sample((R, N, N)) < DENSITY, np.eye(N)[None]))
    base = f32(np.random.standard_normal((C, S)))
    return {"x": x, "w": w, "att_self": att_self, "att_neigh": att_neigh, "b": b, "adj_t": adj_t, "base": base, "offs": striped(np.random.permutation(S)[:N])}


def reference(x, w, att_self, att_neigh, b, adj_t, base, offs):
    idx = offs[:16].T.reshape(-1)
    feat = (f64(w).T @ f64(x)).reshape(H, D, N)
    s = np.sum(feat * f64(att_self).reshape(H, D, 1), axis=1)
    t = np.sum(feat * f64(att_neigh).reshape(H, D, 1), axis=1)
    bias = f64(b).reshape(H, D, 1)
    adj = f64(adj_t)
    val = np.zeros((R, H, D, N))
    for h in range(H):
        v = t[h][:, None] + s[h][None, :]
        p = np.exp(np.maximum(v, SLOPE * v))[None] * adj
        den = np.sum(p, axis=1)[:, None, :]
        num = np.matmul(feat[h][None], p)
        val[:, h] = np.maximum(num + bias[h][None] * den, 0.0) * (1.0 / den)
    res = f64(base).copy()
    res[:, idx] = val.reshape(C, N)
    return res

@@ -1,0 +1,154 @@
+from contextlib import ExitStack
+
+import concourse.mybir as mybir
+from concourse.masks import make_identity
+
+F32, BF16, U16 = mybir.dt.float32, mybir.dt.bfloat16, mybir.dt.uint16
+FN = mybir.ActivationFunctionType
+ALU = mybir.AluOpType
+
+P = 128
+F, H, R, N, S = 512, 4, 2, 1024, 2048
+M = H * P
+FB = F // P
+UB = N // P
+W = 512
+JH = N // W
+SLOPE = 0.2
+
+FLOPS = 2 * F * M * N + 4 * M * N + 2 * R * M * N * N + 2 * R * H * N * N
+
+
+def tile_mgatlayer_b_kernel(tc, x, w, att_self, att_neigh, b, adj_t, base, offs, out):
+    nc = tc.nc
+    with ExitStack() as ctx:
+        held = ctx.enter_context(tc.tile_pool(name="held", bufs=1))
+        head = ctx.enter_context(tc.tile_pool(name="head", bufs=2))
+        ring = ctx.enter_context(tc.tile_pool(name="ring", bufs=3))
+        prep = ctx.enter_context(tc.psum_pool(name="prep", bufs=2))
+        acc = ctx.enter_context(tc.psum_pool(name="acc", bufs=6))
+
+        offsets = held.tile([P, N // 16], U16, name="offsets")
+        nc.sync.dma_start(offsets[:], offs)
+        w_sb = held.tile([P, FB, M], BF16, name="w_sb")
+        x_sb = held.tile([P, FB, N], BF16, name="x_sb")
+        for k in range(FB):
+            nc.sync.dma_start(w_sb[:, k, :], w[k * P : (k + 1) * P, :])
+            nc.sync.dma_start(x_sb[:, k, :], x[k * P : (k + 1) * P, :])
+        att_rows = held.tile([P, P], BF16, name="att_rows")
+        b_rows = held.tile([P, P], F32, name="b_rows")
+        nc.vector.memset(att_rows[:], 0.0)
+        nc.vector.memset(b_rows[:], 0.0)
+        nc.sync.dma_start(att_rows[0:H, :], att_self.rearrange("(h d) o -> h (d o)", d=P))
+        nc.sync.dma_start(att_rows[H : 2 * H, :], att_neigh.rearrange("(h d) o -> h (d o)", d=P))
+        nc.sync.dma_start(b_rows[0:H, :], b.rearrange("(h d) o -> h (d o)", d=P))
+        adj = []
+        for ub in range(UB):
+            adj_ub = held.tile([P, R, N], BF16, name=f"adj{ub}")
+            for r in range(R):
+                nc.sync.dma_start(adj_ub[:, r, :], adj_t[r, ub * P : (ub + 1) * P, :])
+            adj.append(adj_ub)
+        window = {}
+        for h in range(H):
+            for r in range(R):
+                window[r, h] = held.tile([P, S], F32, name=f"window{r}{h}")
+                row = r * M + h * P
+                nc.sync.dma_start(window[r, h][:], base[row : row + P, :])
+
+        ident_bf = held.tile([P, P], BF16, name="ident_bf")
+        ident_f32 = held.tile([P, P], F32, name="ident_f32")
+        make_identity(nc, ident_bf[:])
+        make_identity(nc, ident_f32[:])
+        ones = held.tile([P, P], BF16, name="ones")
+        nc.vector.memset(ones[:], 1.0)
+
+        att_ps = prep.tile([P, P], BF16, tag="prep", name="att_ps")
+        nc.tensor.transpose(att_ps[:], att_rows[:], ident_bf[:])
+        att_cols = held.tile([P, 2 * H], BF16, name="att_cols")
+        nc.vector.tensor_copy(att_cols[:], att_ps[:, 0 : 2 * H])
+        b_ps = prep.tile([P, P], F32, tag="prep", name="b_ps")
+        nc.tensor.transpose(b_ps[:], b_rows[:], ident_f32[:])
+        b_cols = held.tile([P, H], F32, name="b_cols")
+        nc.vector.tensor_copy(b_cols[:], b_ps[:, 0:H])
+        att_self_rep = held.tile([P, H, P], BF16, name="att_self_rep")
+        nc.vector.tensor_copy(att_self_rep[:], att_cols[:, 0:H].unsqueeze(2).to_broadcast([P, H, P]))
+
+        def prepare(h):
+            feat = head.tile([P, N], BF16, name="feat")
+            for jh in range(JH):
+                feat_ps = prep.tile([P, W], F32, tag="prep", name="feat_ps")
+                for k in range(FB):
+                    nc.tensor.matmul(
+                        feat_ps[:],
+                        w_sb[:, k, h * P : (h + 1) * P],
+                        x_sb[:, k, jh * W : (jh + 1) * W],
+                        start=(k == 0),
+                        stop=(k == FB - 1),
+                    )
+                nc.scalar.copy(feat[:, jh * W : (jh + 1) * W], feat_ps[:])
+
+            feat_t_ps = prep.tile([P, UB, P], BF16, tag="prep", name="feat_t_ps")
+            t_ps = prep.tile([P, UB], F32, tag="prep", name="t_ps")
+            for ub in range(UB):
+                block = feat[:, ub * P : (ub + 1) * P]
+                nc.tensor.transpose(feat_t_ps[:, ub, :], block, ident_bf[:])
+                nc.tensor.matmul(t_ps[:, ub : ub + 1], block, att_cols[:, H + h : H + h + 1], start=True, stop=True)
+            feat_t = head.tile([P, UB, P], BF16, name="feat_t")
+            nc.vector.tensor_copy(feat_t[:], feat_t_ps[:])
+            t_steep = head.tile([P, UB], F32, name="t_steep")
+            t_flat = head.tile([P, UB], F32, name="t_flat")
+            nc.vector.tensor_scalar_mul(t_steep[:], t_ps[:], 1.0 - SLOPE)
+            nc.vector.tensor_scalar_mul(t_flat[:], t_ps[:], SLOPE)
+
+            s_rows = head.tile([P, N], F32, name="s_rows")
+            for jh in range(JH):
+                s_ps = prep.tile([P, W], F32, tag="prep", name="s_ps")
+                nc.tensor.matmul(s_ps[:], att_self_rep[:, h, :], feat[:, jh * W : (jh + 1) * W], start=True, stop=True)
+                nc.scalar.copy(s_rows[:, jh * W : (jh + 1) * W], s_ps[:])
+            return feat_t, t_steep, t_flat, s_rows
+
+        def sums_over_neighbours(h, jh, prepared):
+            feat_t, t_steep, t_flat, s_rows = prepared
+            cols = slice(jh * W, (jh + 1) * W)
+            num = [acc.tile([P, W], F32, tag="acc", name=f"num{r}") for r in range(R)]
+            den = [acc.tile([P, W], F32, tag="acc", name=f"den{r}") for r in range(R)]
+            for ub in range(UB):
+                first, last = ub == 0, ub == UB - 1
+                steep = ring.tile([P, W], F32, name="steep")
+                nc.scalar.activation(steep[:], s_rows[:, cols], FN.Relu, bias=t_steep[:, ub : ub + 1], scale=1.0 - SLOPE)
+                e = ring.tile([P, W], BF16, name="e", bufs=8)
+                nc.scalar.activation(e[:], steep[:], FN.Exp, bias=t_flat[:, ub : ub + 1], scale=1.0)
+                p = ring.tile([P, R, W], BF16, name="p", bufs=6)
+                nc.vector.tensor_tensor(p[:], e[:].unsqueeze(1).to_broadcast([P, R, W]), adj[ub][:, :, cols], ALU.mult)
+                for r in range(R):
+                    nc.tensor.matmul(num[r][:], feat_t[:, ub, :], p[:, r, :], start=first, stop=last)
+                for r in range(R):
+                    nc.tensor.matmul(den[r][:], ones[:], p[:, r, :], start=first, stop=last)
+            return num, den
+
+        def place(h, jh, num, den):
+            piece = offsets[:, jh * (W // 16) : (jh + 1) * (W // 16)]
+            for r in range(R):
+                b_den = ring.tile([P, W], F32, name="b_den")
+                nc.scalar.activation(b_den[:], den[r][:], FN.Identity, scale=b_cols[:, h : h + 1])
+                ln_den = ring.tile([P, W], F32, name="ln_den")
+                nc.scalar.activation(ln_den[:], den[r][:], FN.Ln)
+                inv_den = ring.tile([P, W], F32, name="inv_den")
+                nc.scalar.activation(inv_den[:], ln_den[:], FN.Exp, scale=-1.0)
+                biased = ring.tile([P, W], F32, name="biased")
+                nc.vector.tensor_tensor(biased[:], num[r][:], b_den[:], ALU.add)
+                positive = ring.tile([P, W], F32, name="positive")
+                nc.vector.tensor_scalar_max(positive[:], biased[:], 0.0)
+                nc.vector.tensor_tensor(window[r, h][:].indirect(piece), positive[:], inv_den[:], ALU.mult)
+
+        prepared = prepare(0)
+        for h in range(H):
+            for jh in range(JH):
+                num, den = sums_over_neighbours(h, jh, prepared)
+                if jh == 0 and h + 1 < H:
+                    following = prepare(h + 1)
+                place(h, jh, num, den)
+            for r in range(R):
+                row = r * M + h * P
+                nc.sync.dma_start(out[row : row + P, :], window[r, h][:])
+            prepared = following

@@ -129,14 +129,24 @@ def tile_mgatlayer_b_kernel(tc, x, w, att_self, att_neigh, b, adj_t, base, offs,
         def place(h, jh, num, den):
             piece = offsets[:, jh * (W // 16) : (jh + 1) * (W // 16)]
             for r in range(R):
-                b_den = ring.tile([P, W], F32, name="b_den")
-                nc.scalar.activation(b_den[:], den[r][:], FN.Identity, scale=b_cols[:, h : h + 1])
-                ln_den = ring.tile([P, W], F32, name="ln_den")
-                nc.scalar.activation(ln_den[:], den[r][:], FN.Ln)
-                inv_den = ring.tile([P, W], F32, name="inv_den")
-                nc.scalar.activation(inv_den[:], ln_den[:], FN.Exp, scale=-1.0)
+                den_rows = ring.tile([P, W], F32, name="den_rows")
+                nc.scalar.copy(den_rows[:], den[r][:])
                 biased = ring.tile([P, W], F32, name="biased")
-                nc.vector.tensor_tensor(biased[:], num[r][:], b_den[:], ALU.add)
+                nc.vector.scalar_tensor_tensor(
+                    biased[:], den_rows[:], b_cols[:, h : h + 1], num[r][:], op0=ALU.mult, op1=ALU.add
+                )
+                den_cols_ps = prep.tile([P, W // P, P], F32, tag="prep", name="den_cols_ps")
+                for q in range(W // P):
+                    nc.tensor.transpose(den_cols_ps[:, q, :], den_rows[:, q * P : (q + 1) * P], ident_f32[:])
+                inv_cols = ring.tile([P, W // P], F32, name="inv_cols")
+                nc.vector.reciprocal(inv_cols[:], den_cols_ps[:, :, 0])
+                inv_ps = prep.tile([P, W], F32, tag="prep", name="inv_ps")
+                for q in range(W // P):
+                    nc.tensor.transpose(
+                        inv_ps[:, q * P : (q + 1) * P], inv_cols[:, q : q + 1].to_broadcast([P, P]), ident_f32[:]
+                    )
+                inv_den = ring.tile([P, W], F32, name="inv_den")
+                nc.scalar.copy(inv_den[:], inv_ps[:])
                 positive = ring.tile([P, W], F32, name="positive")
                 nc.vector.tensor_scalar_max(positive[:], biased[:], 0.0)
                 nc.vector.tensor_tensor(window[r, h][:].indirect(piece), positive[:], inv_den[:], ALU.mult)
@@ -146,9 +156,10 @@ def tile_mgatlayer_b_kernel(tc, x, w, att_self, att_neigh, b, adj_t, base, offs,
             for jh in range(JH):
                 num, den = sums_over_neighbours(h, jh, prepared)
                 if jh == 0 and h + 1 < H:
-                    following = prepare(h + 1)
+                    upcoming = prepare(h + 1)
                 place(h, jh, num, den)
             for r in range(R):
                 row = r * M + h * P
                 nc.sync.dma_start(out[row : row + P, :], window[r, h][:])
-            prepared = following
+            if h + 1 < H:
+                prepared = upcoming

@@ -26,15 +26,11 @@ def tile_mgatlayer_b_kernel(tc, x, w, att_self, att_neigh, b, adj_t, base, offs,
         head = ctx.enter_context(tc.tile_pool(name="head", bufs=2))
         ring = ctx.enter_context(tc.tile_pool(name="ring", bufs=3))
         prep = ctx.enter_context(tc.psum_pool(name="prep", bufs=2))
-        acc = ctx.enter_context(tc.psum_pool(name="acc", bufs=6))
+        acc = ctx.enter_context(tc.psum_pool(name="acc", bufs=4))
+        turn = ctx.enter_context(tc.psum_pool(name="turn", bufs=2))
 
         offsets = held.tile([P, N // 16], U16, name="offsets")
         nc.sync.dma_start(offsets[:], offs)
-        w_sb = held.tile([P, FB, M], BF16, name="w_sb")
-        x_sb = held.tile([P, FB, N], BF16, name="x_sb")
-        for k in range(FB):
-            nc.sync.dma_start(w_sb[:, k, :], w[k * P : (k + 1) * P, :])
-            nc.sync.dma_start(x_sb[:, k, :], x[k * P : (k + 1) * P, :])
         att_rows = held.tile([P, P], BF16, name="att_rows")
         b_rows = held.tile([P, P], F32, name="b_rows")
         nc.vector.memset(att_rows[:], 0.0)
@@ -42,6 +38,11 @@ def tile_mgatlayer_b_kernel(tc, x, w, att_self, att_neigh, b, adj_t, base, offs,
         nc.sync.dma_start(att_rows[0:H, :], att_self.rearrange("(h d) o -> h (d o)", d=P))
         nc.sync.dma_start(att_rows[H : 2 * H, :], att_neigh.rearrange("(h d) o -> h (d o)", d=P))
         nc.sync.dma_start(b_rows[0:H, :], b.rearrange("(h d) o -> h (d o)", d=P))
+        w_sb = held.tile([P, FB, M], BF16, name="w_sb")
+        x_sb = held.tile([P, FB, N], BF16, name="x_sb")
+        for k in range(FB):
+            nc.sync.dma_start(w_sb[:, k, :], w[k * P : (k + 1) * P, :])
+            nc.sync.dma_start(x_sb[:, k, :], x[k * P : (k + 1) * P, :])
         adj = []
         for ub in range(UB):
             adj_ub = held.tile([P, R, N], BF16, name=f"adj{ub}")
@@ -75,91 +76,108 @@ def tile_mgatlayer_b_kernel(tc, x, w, att_self, att_neigh, b, adj_t, base, offs,
 
         def prepare(h):
             feat = head.tile([P, N], BF16, name="feat")
-            for jh in range(JH):
-                feat_ps = prep.tile([P, W], F32, tag="prep", name="feat_ps")
-                for k in range(FB):
+            feat_ps = [prep.tile([P, W], F32, tag="prep", name=f"feat_ps{jh}") for jh in range(JH)]
+            for k in range(FB):
+                for jh in range(JH):
                     nc.tensor.matmul(
-                        feat_ps[:],
+                        feat_ps[jh][:],
                         w_sb[:, k, h * P : (h + 1) * P],
                         x_sb[:, k, jh * W : (jh + 1) * W],
                         start=(k == 0),
                         stop=(k == FB - 1),
                     )
-                nc.scalar.copy(feat[:, jh * W : (jh + 1) * W], feat_ps[:])
-
-            feat_t_ps = prep.tile([P, UB, P], BF16, tag="prep", name="feat_t_ps")
-            t_ps = prep.tile([P, UB], F32, tag="prep", name="t_ps")
-            for ub in range(UB):
-                block = feat[:, ub * P : (ub + 1) * P]
-                nc.tensor.transpose(feat_t_ps[:, ub, :], block, ident_bf[:])
-                nc.tensor.matmul(t_ps[:, ub : ub + 1], block, att_cols[:, H + h : H + h + 1], start=True, stop=True)
-            feat_t = head.tile([P, UB, P], BF16, name="feat_t")
-            nc.vector.tensor_copy(feat_t[:], feat_t_ps[:])
-            t_steep = head.tile([P, UB], F32, name="t_steep")
-            t_flat = head.tile([P, UB], F32, name="t_flat")
-            nc.vector.tensor_scalar_mul(t_steep[:], t_ps[:], 1.0 - SLOPE)
-            nc.vector.tensor_scalar_mul(t_flat[:], t_ps[:], SLOPE)
+            for jh in range(JH):
+                nc.scalar.copy(feat[:, jh * W : (jh + 1) * W], feat_ps[jh][:])
 
             s_rows = head.tile([P, N], F32, name="s_rows")
             for jh in range(JH):
                 s_ps = prep.tile([P, W], F32, tag="prep", name="s_ps")
                 nc.tensor.matmul(s_ps[:], att_self_rep[:, h, :], feat[:, jh * W : (jh + 1) * W], start=True, stop=True)
                 nc.scalar.copy(s_rows[:, jh * W : (jh + 1) * W], s_ps[:])
+
+            t_ps = prep.tile([P, UB], F32, tag="prep", name="t_ps")
+            for ub in range(UB):
+                nc.tensor.matmul(
+                    t_ps[:, ub : ub + 1], feat[:, ub * P : (ub + 1) * P], att_cols[:, H + h : H + h + 1], start=True, stop=True
+                )
+            t_steep = head.tile([P, UB], F32, name="t_steep")
+            t_flat = head.tile([P, UB], F32, name="t_flat")
+            nc.vector.tensor_scalar_mul(t_steep[:], t_ps[:], 1.0 - SLOPE)
+            nc.vector.tensor_scalar_mul(t_flat[:], t_ps[:], SLOPE)
+            feat_t_ps = prep.tile([P, UB, P], BF16, tag="prep", name="feat_t_ps")
+            for ub in range(UB):
+                nc.tensor.transpose(feat_t_ps[:, ub, :], feat[:, ub * P : (ub + 1) * P], ident_bf[:])
+            feat_t = head.tile([P, UB, P], BF16, name="feat_t")
+            nc.vector.tensor_copy(feat_t[:], feat_t_ps[:])
             return feat_t, t_steep, t_flat, s_rows
 
-        def sums_over_neighbours(h, jh, prepared):
+        def attention(jh, prepared):
             feat_t, t_steep, t_flat, s_rows = prepared
-            cols = slice(jh * W, (jh + 1) * W)
-            num = [acc.tile([P, W], F32, tag="acc", name=f"num{r}") for r in range(R)]
-            den = [acc.tile([P, W], F32, tag="acc", name=f"den{r}") for r in range(R)]
+            e_blocks = []
             for ub in range(UB):
-                first, last = ub == 0, ub == UB - 1
                 steep = ring.tile([P, W], F32, name="steep")
-                nc.scalar.activation(steep[:], s_rows[:, cols], FN.Relu, bias=t_steep[:, ub : ub + 1], scale=1.0 - SLOPE)
-                e = ring.tile([P, W], BF16, name="e", bufs=8)
+                nc.scalar.activation(
+                    steep[:], s_rows[:, jh * W : (jh + 1) * W], FN.Relu, bias=t_steep[:, ub : ub + 1], scale=1.0 - SLOPE
+                )
+                e = ring.tile([P, W], BF16, name="e", bufs=2 * UB)
                 nc.scalar.activation(e[:], steep[:], FN.Exp, bias=t_flat[:, ub : ub + 1], scale=1.0)
-                p = ring.tile([P, R, W], BF16, name="p", bufs=6)
-                nc.vector.tensor_tensor(p[:], e[:].unsqueeze(1).to_broadcast([P, R, W]), adj[ub][:, :, cols], ALU.mult)
-                for r in range(R):
-                    nc.tensor.matmul(num[r][:], feat_t[:, ub, :], p[:, r, :], start=first, stop=last)
-                for r in range(R):
-                    nc.tensor.matmul(den[r][:], ones[:], p[:, r, :], start=first, stop=last)
+                e_blocks.append(e)
+            return e_blocks
+
+        def sums_over_neighbours(jh, r, prepared, e_blocks):
+            feat_t = prepared[0]
+            num = acc.tile([P, W], F32, tag="acc", name="num")
+            den = acc.tile([P, W], F32, tag="acc", name="den")
+            for ub in range(UB):
+                p = ring.tile([P, W], BF16, name="p", bufs=2 * UB)
+                nc.vector.tensor_tensor(p[:], e_blocks[ub][:], adj[ub][:, r, jh * W : (jh + 1) * W], ALU.mult)
+                nc.tensor.matmul(num[:], feat_t[:, ub, :], p[:], start=(ub == 0), stop=(ub == UB - 1))
+                nc.tensor.matmul(den[:], ones[:], p[:], start=(ub == 0), stop=(ub == UB - 1))
             return num, den
 
-        def place(h, jh, num, den):
-            piece = offsets[:, jh * (W // 16) : (jh + 1) * (W // 16)]
-            for r in range(R):
-                den_rows = ring.tile([P, W], F32, name="den_rows")
-                nc.scalar.copy(den_rows[:], den[r][:])
-                biased = ring.tile([P, W], F32, name="biased")
-                nc.vector.scalar_tensor_tensor(
-                    biased[:], den_rows[:], b_cols[:, h : h + 1], num[r][:], op0=ALU.mult, op1=ALU.add
-                )
-                den_cols_ps = prep.tile([P, W // P, P], F32, tag="prep", name="den_cols_ps")
-                for q in range(W // P):
-                    nc.tensor.transpose(den_cols_ps[:, q, :], den_rows[:, q * P : (q + 1) * P], ident_f32[:])
-                inv_cols = ring.tile([P, W // P], F32, name="inv_cols")
-                nc.vector.reciprocal(inv_cols[:], den_cols_ps[:, :, 0])
-                inv_ps = prep.tile([P, W], F32, tag="prep", name="inv_ps")
-                for q in range(W // P):
-                    nc.tensor.transpose(
-                        inv_ps[:, q * P : (q + 1) * P], inv_cols[:, q : q + 1].to_broadcast([P, P]), ident_f32[:]
-                    )
-                inv_den = ring.tile([P, W], F32, name="inv_den")
-                nc.scalar.copy(inv_den[:], inv_ps[:])
-                positive = ring.tile([P, W], F32, name="positive")
-                nc.vector.tensor_scalar_max(positive[:], biased[:], 0.0)
-                nc.vector.tensor_tensor(window[r, h][:].indirect(piece), positive[:], inv_den[:], ALU.mult)
+        def begin_placing(h, num, den):
+            den_rows = ring.tile([P, W], F32, name="den_rows")
+            nc.scalar.copy(den_rows[:], den[:])
+            biased = ring.tile([P, W], F32, name="biased")
+            nc.vector.scalar_tensor_tensor(
+                biased[:], den_rows[:], b_cols[:, h : h + 1], num[:], op0=ALU.mult, op1=ALU.add
+            )
+            den_cols_ps = turn.tile([P, W // P, P], F32, tag="turn", name="den_cols_ps")
+            for q in range(W // P):
+                nc.tensor.transpose(den_cols_ps[:, q, :], den_rows[:, q * P : (q + 1) * P], ident_f32[:])
+            inv_cols = ring.tile([P, W // P], F32, name="inv_cols")
+            nc.vector.reciprocal(inv_cols[:], den_cols_ps[:, :, 0])
+            positive = ring.tile([P, W], F32, name="positive")
+            nc.vector.tensor_scalar_max(positive[:], biased[:], 0.0)
+            return positive, inv_cols
 
-        prepared = prepare(0)
-        for h in range(H):
-            for jh in range(JH):
-                num, den = sums_over_neighbours(h, jh, prepared)
-                if jh == 0 and h + 1 < H:
-                    upcoming = prepare(h + 1)
-                place(h, jh, num, den)
-            for r in range(R):
+        def finish_placing(h, jh, r, positive, inv_cols):
+            inv_ps = turn.tile([P, W], F32, tag="turn", name="inv_ps")
+            for q in range(W // P):
+                nc.tensor.transpose(
+                    inv_ps[:, q * P : (q + 1) * P], inv_cols[:, q : q + 1].to_broadcast([P, P]), ident_f32[:]
+                )
+            inv_den = ring.tile([P, W], F32, name="inv_den")
+            nc.scalar.copy(inv_den[:], inv_ps[:])
+            piece = offsets[:, jh * (W // 16) : (jh + 1) * (W // 16)]
+            nc.vector.tensor_tensor(window[r, h][:].indirect(piece), positive[:], inv_den[:], ALU.mult)
+            if jh == JH - 1:
                 row = r * M + h * P
                 nc.sync.dma_start(out[row : row + P, :], window[r, h][:])
+
+        prepared = prepare(0)
+        half_placed = None
+        for h in range(H):
+            for jh in range(JH):
+                e_blocks = attention(jh, prepared)
+                for r in range(R):
+                    if jh == 0 and r == 1 and h + 1 < H:
+                        upcoming = prepare(h + 1)
+                    num, den = sums_over_neighbours(jh, r, prepared, e_blocks)
+                    positive, inv_cols = begin_placing(h, num, den)
+                    if half_placed is not None:
+                        finish_placing(*half_placed)
+                    half_placed = (h, jh, r, positive, inv_cols)
             if h + 1 < H:
                 prepared = upcoming
+        finish_placing(*half_placed)

@@ -14,6 +14,9 @@ FB = F // P
 UB = N // P
 W = 512
 JH = N // W
+QB = W // P
+PAIR = 2
+ROW = 144
 SLOPE = 0.2
 
 FLOPS = 2 * F * M * N + 4 * M * N + 2 * R * M * N * N + 2 * R * H * N * N
@@ -32,17 +35,16 @@ def tile_mgatlayer_b_kernel(tc, x, w, att_self, att_neigh, b, adj_t, base, offs,
         offsets = held.tile([P, N // 16], U16, name="offsets")
         nc.sync.dma_start(offsets[:], offs)
         att_rows = held.tile([P, P], BF16, name="att_rows")
-        b_rows = held.tile([P, P], F32, name="b_rows")
         nc.vector.memset(att_rows[:], 0.0)
-        nc.vector.memset(b_rows[:], 0.0)
         nc.sync.dma_start(att_rows[0:H, :], att_self.rearrange("(h d) o -> h (d o)", d=P))
         nc.sync.dma_start(att_rows[H : 2 * H, :], att_neigh.rearrange("(h d) o -> h (d o)", d=P))
-        nc.sync.dma_start(b_rows[0:H, :], b.rearrange("(h d) o -> h (d o)", d=P))
         w_sb = held.tile([P, FB, M], BF16, name="w_sb")
         x_sb = held.tile([P, FB, N], BF16, name="x_sb")
         for k in range(FB):
             nc.sync.dma_start(w_sb[:, k, :], w[k * P : (k + 1) * P, :])
             nc.sync.dma_start(x_sb[:, k, :], x[k * P : (k + 1) * P, :])
+        b_rows = held.tile([P, M], F32, name="b_rows")
+        nc.sync.dma_start(b_rows[:], b.rearrange("m o -> (m o)").partition_broadcast(P))
         adj = []
         for ub in range(UB):
             adj_ub = held.tile([P, R, N], BF16, name=f"adj{ub}")
@@ -60,17 +62,14 @@ def tile_mgatlayer_b_kernel(tc, x, w, att_self, att_neigh, b, adj_t, base, offs,
         ident_f32 = held.tile([P, P], F32, name="ident_f32")
         make_identity(nc, ident_bf[:])
         make_identity(nc, ident_f32[:])
-        ones = held.tile([P, P], BF16, name="ones")
-        nc.vector.memset(ones[:], 1.0)
+        feat_aug = [held.tile([P, UB, ROW], BF16, name=f"feat_aug{i}") for i in range(2)]
+        for i in range(2):
+            nc.gpsimd.memset(feat_aug[i][:, :, P:ROW], 1.0)
 
         att_ps = prep.tile([P, P], BF16, tag="prep", name="att_ps")
         nc.tensor.transpose(att_ps[:], att_rows[:], ident_bf[:])
         att_cols = held.tile([P, 2 * H], BF16, name="att_cols")
         nc.vector.tensor_copy(att_cols[:], att_ps[:, 0 : 2 * H])
-        b_ps = prep.tile([P, P], F32, tag="prep", name="b_ps")
-        nc.tensor.transpose(b_ps[:], b_rows[:], ident_f32[:])
-        b_cols = held.tile([P, H], F32, name="b_cols")
-        nc.vector.tensor_copy(b_cols[:], b_ps[:, 0:H])
         att_self_rep = held.tile([P, H, P], BF16, name="att_self_rep")
         nc.vector.tensor_copy(att_self_rep[:], att_cols[:, 0:H].unsqueeze(2).to_broadcast([P, H, P]))
 
@@ -104,56 +103,67 @@ def tile_mgatlayer_b_kernel(tc, x, w, att_self, att_neigh, b, adj_t, base, offs,
             t_flat = head.tile([P, UB], F32, name="t_flat")
             nc.vector.tensor_scalar_mul(t_steep[:], t_ps[:], 1.0 - SLOPE)
             nc.vector.tensor_scalar_mul(t_flat[:], t_ps[:], SLOPE)
+
             feat_t_ps = prep.tile([P, UB, P], BF16, tag="prep", name="feat_t_ps")
             for ub in range(UB):
                 nc.tensor.transpose(feat_t_ps[:, ub, :], feat[:, ub * P : (ub + 1) * P], ident_bf[:])
-            feat_t = head.tile([P, UB, P], BF16, name="feat_t")
-            nc.vector.tensor_copy(feat_t[:], feat_t_ps[:])
-            return feat_t, t_steep, t_flat, s_rows
+            nc.vector.tensor_copy(feat_aug[h % 2][:, :, 0:P], feat_t_ps[:])
+            return t_steep, t_flat, s_rows
 
         def attention(jh, prepared):
-            feat_t, t_steep, t_flat, s_rows = prepared
-            e_blocks = []
+            t_steep, t_flat, s_rows = prepared
+            p_blocks = []
             for ub in range(UB):
                 steep = ring.tile([P, W], F32, name="steep")
                 nc.scalar.activation(
                     steep[:], s_rows[:, jh * W : (jh + 1) * W], FN.Relu, bias=t_steep[:, ub : ub + 1], scale=1.0 - SLOPE
                 )
-                e = ring.tile([P, W], BF16, name="e", bufs=2 * UB)
+                e = ring.tile([P, W], BF16, name="e", bufs=4)
                 nc.scalar.activation(e[:], steep[:], FN.Exp, bias=t_flat[:, ub : ub + 1], scale=1.0)
-                e_blocks.append(e)
-            return e_blocks
+                p = ring.tile([P, R, W], BF16, name="p", bufs=2 * UB)
+                nc.vector.tensor_tensor(
+                    p[:], e[:].unsqueeze(1).to_broadcast([P, R, W]), adj[ub][:, :, jh * W : (jh + 1) * W], ALU.mult
+                )
+                p_blocks.append(p)
+            return p_blocks
 
-        def sums_over_neighbours(jh, r, prepared, e_blocks):
-            feat_t = prepared[0]
-            num = acc.tile([P, W], F32, tag="acc", name="num")
-            den = acc.tile([P, W], F32, tag="acc", name="den")
-            for ub in range(UB):
-                p = ring.tile([P, W], BF16, name="p", bufs=2 * UB)
-                nc.vector.tensor_tensor(p[:], e_blocks[ub][:], adj[ub][:, r, jh * W : (jh + 1) * W], ALU.mult)
-                nc.tensor.matmul(num[:], feat_t[:, ub, :], p[:], start=(ub == 0), stop=(ub == UB - 1))
-                nc.tensor.matmul(den[:], ones[:], p[:], start=(ub == 0), stop=(ub == UB - 1))
-            return num, den
+        def sums_over_neighbours(h, r, p_blocks):
+            sums = [acc.tile([P, PAIR, P + 1], F32, tag="acc", name=f"sums{i}") for i in range(QB // PAIR)]
+            for q in range(QB):
+                for ub in range(UB):
+                    nc.tensor.matmul(
+                        sums[q // PAIR][:, q % PAIR, :],
+                        p_blocks[ub][:, r, q * P : (q + 1) * P],
+                        feat_aug[h % 2][:, ub, 0 : P + 1],
+                        start=(ub == 0),
+                        stop=(ub == UB - 1),
+                    )
+            return sums
 
-        def begin_placing(h, num, den):
-            den_rows = ring.tile([P, W], F32, name="den_rows")
-            nc.scalar.copy(den_rows[:], den[:])
-            biased = ring.tile([P, W], F32, name="biased")
-            nc.vector.scalar_tensor_tensor(
-                biased[:], den_rows[:], b_cols[:, h : h + 1], num[:], op0=ALU.mult, op1=ALU.add
-            )
-            den_cols_ps = turn.tile([P, W // P, P], F32, tag="turn", name="den_cols_ps")
-            for q in range(W // P):
-                nc.tensor.transpose(den_cols_ps[:, q, :], den_rows[:, q * P : (q + 1) * P], ident_f32[:])
-            inv_cols = ring.tile([P, W // P], F32, name="inv_cols")
-            nc.vector.reciprocal(inv_cols[:], den_cols_ps[:, :, 0])
+        def begin_placing(h, sums):
+            inv_cols = ring.tile([P, QB], F32, name="inv_cols")
+            biased_t = ring.tile([P, QB, P], F32, name="biased_t")
+            for i in range(QB // PAIR):
+                nc.vector.reciprocal(inv_cols[:, i * PAIR : (i + 1) * PAIR], sums[i][:, :, P])
+            for q in range(QB):
+                nc.vector.scalar_tensor_tensor(
+                    biased_t[:, q, :],
+                    b_rows[:, h * P : (h + 1) * P],
+                    sums[q // PAIR][:, q % PAIR, P : P + 1],
+                    sums[q // PAIR][:, q % PAIR, 0:P],
+                    op0=ALU.mult,
+                    op1=ALU.add,
+                )
+            return biased_t, inv_cols
+
+        def finish_placing(h, jh, r, biased_t, inv_cols):
+            biased_ps = turn.tile([P, W], F32, tag="turn", name="biased_ps")
+            for q in range(QB):
+                nc.tensor.transpose(biased_ps[:, q * P : (q + 1) * P], biased_t[:, q, :], ident_f32[:])
             positive = ring.tile([P, W], F32, name="positive")
-            nc.vector.tensor_scalar_max(positive[:], biased[:], 0.0)
-            return positive, inv_cols
-
-        def finish_placing(h, jh, r, positive, inv_cols):
+            nc.scalar.activation(positive[:], biased_ps[:], FN.Relu)
             inv_ps = turn.tile([P, W], F32, tag="turn", name="inv_ps")
-            for q in range(W // P):
+            for q in range(QB):
                 nc.tensor.transpose(
                     inv_ps[:, q * P : (q + 1) * P], inv_cols[:, q : q + 1].to_broadcast([P, P]), ident_f32[:]
                 )
@@ -169,15 +179,15 @@ def tile_mgatlayer_b_kernel(tc, x, w, att_self, att_neigh, b, adj_t, base, offs,
         half_placed = None
         for h in range(H):
             for jh in range(JH):
-                e_blocks = attention(jh, prepared)
+                p_blocks = attention(jh, prepared)
                 for r in range(R):
                     if jh == 0 and r == 1 and h + 1 < H:
                         upcoming = prepare(h + 1)
-                    num, den = sums_over_neighbours(jh, r, prepared, e_blocks)
-                    positive, inv_cols = begin_placing(h, num, den)
+                    sums = sums_over_neighbours(h, r, p_blocks)
+                    biased_t, inv_cols = begin_placing(h, sums)
                     if half_placed is not None:
                         finish_placing(*half_placed)
-                    half_placed = (h, jh, r, positive, inv_cols)
+                    half_placed = (h, jh, r, biased_t, inv_cols)
             if h + 1 < H:
                 prepared = upcoming
         finish_placing(*half_placed)

@@ -12,6 +12,7 @@ F, H, R, N, S = 512, 4, 2, 1024, 2048
 M = H * P
 FB = F // P
 UB = N // P
+UP = 2
 W = 512
 JH = N // W
 QB = W // P
@@ -46,11 +47,13 @@ def tile_mgatlayer_b_kernel(tc, x, w, att_self, att_neigh, b, adj_t, base, offs,
         b_rows = held.tile([P, M], F32, name="b_rows")
         nc.sync.dma_start(b_rows[:], b.rearrange("m o -> (m o)").partition_broadcast(P))
         adj = []
-        for ub in range(UB):
-            adj_ub = held.tile([P, R, N], BF16, name=f"adj{ub}")
-            for r in range(R):
-                nc.sync.dma_start(adj_ub[:, r, :], adj_t[r, ub * P : (ub + 1) * P, :])
-            adj.append(adj_ub)
+        for g in range(UB // UP):
+            adj_g = held.tile([P, UP, R, N], BF16, name=f"adj{g}")
+            for i in range(UP):
+                for r in range(R):
+                    first = (g * UP + i) * P
+                    nc.sync.dma_start(adj_g[:, i, r, :], adj_t[r, first : first + P, :])
+            adj.append(adj_g)
         window = {}
         for h in range(H):
             for r in range(R):
@@ -112,28 +115,30 @@ def tile_mgatlayer_b_kernel(tc, x, w, att_self, att_neigh, b, adj_t, base, offs,
 
         def attention(jh, prepared):
             t_steep, t_flat, s_rows = prepared
-            p_blocks = []
-            for ub in range(UB):
-                steep = ring.tile([P, W], F32, name="steep")
-                nc.scalar.activation(
-                    steep[:], s_rows[:, jh * W : (jh + 1) * W], FN.Relu, bias=t_steep[:, ub : ub + 1], scale=1.0 - SLOPE
-                )
-                e = ring.tile([P, W], BF16, name="e", bufs=4)
-                nc.scalar.activation(e[:], steep[:], FN.Exp, bias=t_flat[:, ub : ub + 1], scale=1.0)
-                p = ring.tile([P, R, W], BF16, name="p", bufs=2 * UB)
+            p_groups = []
+            for g in range(UB // UP):
+                e = ring.tile([P, UP, W], BF16, name="e")
+                for i in range(UP):
+                    ub = g * UP + i
+                    steep = ring.tile([P, W], F32, name="steep")
+                    nc.scalar.activation(
+                        steep[:], s_rows[:, jh * W : (jh + 1) * W], FN.Relu, bias=t_steep[:, ub : ub + 1], scale=1.0 - SLOPE
+                    )
+                    nc.scalar.activation(e[:, i, :], steep[:], FN.Exp, bias=t_flat[:, ub : ub + 1], scale=1.0)
+                p = ring.tile([P, UP, R, W], BF16, name="p", bufs=2 * UB // UP)
                 nc.vector.tensor_tensor(
-                    p[:], e[:].unsqueeze(1).to_broadcast([P, R, W]), adj[ub][:, :, jh * W : (jh + 1) * W], ALU.mult
+                    p[:], e[:].unsqueeze(2).to_broadcast([P, UP, R, W]), adj[g][:, :, :, jh * W : (jh + 1) * W], ALU.mult
                 )
-                p_blocks.append(p)
-            return p_blocks
+                p_groups.append(p)
+            return p_groups
 
-        def sums_over_neighbours(h, r, p_blocks):
+        def sums_over_neighbours(h, r, p_groups):
             sums = [acc.tile([P, PAIR, P + 1], F32, tag="acc", name=f"sums{i}") for i in range(QB // PAIR)]
             for q in range(QB):
                 for ub in range(UB):
                     nc.tensor.matmul(
                         sums[q // PAIR][:, q % PAIR, :],
-                        p_blocks[ub][:, r, q * P : (q + 1) * P],
+                        p_groups[ub // UP][:, ub % UP, r, q * P : (q + 1) * P],
                         feat_aug[h % 2][:, ub, 0 : P + 1],
                         start=(ub == 0),
                         stop=(ub == UB - 1),
@@ -179,11 +184,11 @@ def tile_mgatlayer_b_kernel(tc, x, w, att_self, att_neigh, b, adj_t, base, offs,
         half_placed = None
         for h in range(H):
             for jh in range(JH):
-                p_blocks = attention(jh, prepared)
+                p_groups = attention(jh, prepared)
                 for r in range(R):
                     if jh == 0 and r == 1 and h + 1 < H:
                         upcoming = prepare(h + 1)
-                    sums = sums_over_neighbours(h, r, p_blocks)
+                    sums = sums_over_neighbours(h, r, p_groups)
                     biased_t, inv_cols = begin_placing(h, sums)
                     if half_placed is not None:
                         finish_placing(*half_placed)

@@ -12,7 +12,6 @@ F, H, R, N, S = 512, 4, 2, 1024, 2048
 M = H * P
 FB = F // P
 UB = N // P
-UP = 2
 W = 512
 JH = N // W
 QB = W // P
@@ -47,13 +46,11 @@ def tile_mgatlayer_b_kernel(tc, x, w, att_self, att_neigh, b, adj_t, base, offs,
         b_rows = held.tile([P, M], F32, name="b_rows")
         nc.sync.dma_start(b_rows[:], b.rearrange("m o -> (m o)").partition_broadcast(P))
         adj = []
-        for g in range(UB // UP):
-            adj_g = held.tile([P, UP, R, N], BF16, name=f"adj{g}")
-            for i in range(UP):
-                for r in range(R):
-                    first = (g * UP + i) * P
-                    nc.sync.dma_start(adj_g[:, i, r, :], adj_t[r, first : first + P, :])
-            adj.append(adj_g)
+        for ub in range(UB):
+            adj_ub = held.tile([P, R, N], BF16, name=f"adj{ub}")
+            for r in range(R):
+                nc.sync.dma_start(adj_ub[:, r, :], adj_t[r, ub * P : (ub + 1) * P, :])
+            adj.append(adj_ub)
         window = {}
         for h in range(H):
             for r in range(R):
@@ -91,11 +88,11 @@ def tile_mgatlayer_b_kernel(tc, x, w, att_self, att_neigh, b, adj_t, base, offs,
             for jh in range(JH):
                 nc.scalar.copy(feat[:, jh * W : (jh + 1) * W], feat_ps[jh][:])
 
-            s_rows = head.tile([P, N], F32, name="s_rows")
+            s_steep = head.tile([P, N], F32, name="s_steep")
             for jh in range(JH):
                 s_ps = prep.tile([P, W], F32, tag="prep", name="s_ps")
                 nc.tensor.matmul(s_ps[:], att_self_rep[:, h, :], feat[:, jh * W : (jh + 1) * W], start=True, stop=True)
-                nc.scalar.copy(s_rows[:, jh * W : (jh + 1) * W], s_ps[:])
+                nc.scalar.mul(s_steep[:, jh * W : (jh + 1) * W], s_ps[:], 1.0 - SLOPE)
 
             t_ps = prep.tile([P, UB], F32, tag="prep", name="t_ps")
             for ub in range(UB):
@@ -111,34 +108,35 @@ def tile_mgatlayer_b_kernel(tc, x, w, att_self, att_neigh, b, adj_t, base, offs,
             for ub in range(UB):
                 nc.tensor.transpose(feat_t_ps[:, ub, :], feat[:, ub * P : (ub + 1) * P], ident_bf[:])
             nc.vector.tensor_copy(feat_aug[h % 2][:, :, 0:P], feat_t_ps[:])
-            return t_steep, t_flat, s_rows
+            return t_steep, t_flat, s_steep
 
-        def attention(jh, prepared):
-            t_steep, t_flat, s_rows = prepared
-            p_groups = []
-            for g in range(UB // UP):
-                e = ring.tile([P, UP, W], BF16, name="e")
-                for i in range(UP):
-                    ub = g * UP + i
-                    steep = ring.tile([P, W], F32, name="steep")
-                    nc.scalar.activation(
-                        steep[:], s_rows[:, jh * W : (jh + 1) * W], FN.Relu, bias=t_steep[:, ub : ub + 1], scale=1.0 - SLOPE
+        def attention(jh, prepared, relu_on_vector):
+            t_steep, t_flat, s_steep = prepared
+            p_blocks = []
+            for ub in range(UB):
+                steep = ring.tile([P, W], F32, name="steep")
+                if relu_on_vector:
+                    nc.vector.tensor_scalar(
+                        steep[:], s_steep[:, jh * W : (jh + 1) * W], t_steep[:, ub : ub + 1], 0.0, op0=ALU.add, op1=ALU.max
                     )
-                    nc.scalar.activation(e[:, i, :], steep[:], FN.Exp, bias=t_flat[:, ub : ub + 1], scale=1.0)
-                p = ring.tile([P, UP, R, W], BF16, name="p", bufs=2 * UB // UP)
+                else:
+                    nc.scalar.activation(steep[:], s_steep[:, jh * W : (jh + 1) * W], FN.Relu, bias=t_steep[:, ub : ub + 1])
+                e = ring.tile([P, W], BF16, name="e", bufs=4)
+                nc.scalar.activation(e[:], steep[:], FN.Exp, bias=t_flat[:, ub : ub + 1], scale=1.0)
+                p = ring.tile([P, R, W], BF16, name="p", bufs=2 * UB)
                 nc.vector.tensor_tensor(
-                    p[:], e[:].unsqueeze(2).to_broadcast([P, UP, R, W]), adj[g][:, :, :, jh * W : (jh + 1) * W], ALU.mult
+                    p[:], e[:].unsqueeze(1).to_broadcast([P, R, W]), adj[ub][:, :, jh * W : (jh + 1) * W], ALU.mult
                 )
-                p_groups.append(p)
-            return p_groups
+                p_blocks.append(p)
+            return p_blocks
 
-        def sums_over_neighbours(h, r, p_groups):
+        def sums_over_neighbours(h, r, p_blocks):
             sums = [acc.tile([P, PAIR, P + 1], F32, tag="acc", name=f"sums{i}") for i in range(QB // PAIR)]
             for q in range(QB):
                 for ub in range(UB):
                     nc.tensor.matmul(
                         sums[q // PAIR][:, q % PAIR, :],
-                        p_groups[ub // UP][:, ub % UP, r, q * P : (q + 1) * P],
+                        p_blocks[ub][:, r, q * P : (q + 1) * P],
                         feat_aug[h % 2][:, ub, 0 : P + 1],
                         start=(ub == 0),
                         stop=(ub == UB - 1),
@@ -184,11 +182,11 @@ def tile_mgatlayer_b_kernel(tc, x, w, att_self, att_neigh, b, adj_t, base, offs,
         half_placed = None
         for h in range(H):
             for jh in range(JH):
-                p_groups = attention(jh, prepared)
+                p_blocks = attention(jh, prepared, relu_on_vector=(h == 0 and jh == 0))
                 for r in range(R):
                     if jh == 0 and r == 1 and h + 1 < H:
                         upcoming = prepare(h + 1)
-                    sums = sums_over_neighbours(h, r, p_groups)
+                    sums = sums_over_neighbours(h, r, p_blocks)
                     biased_t, inv_cols = begin_placing(h, sums)
                     if half_placed is not None:
                         finish_placing(*half_placed)

@@ -15,8 +15,7 @@ UB = N // P
 W = 512
 JH = N // W
 QB = W // P
-PAIR = 2
-ROW = 144
+PASSES = H * JH
 SLOPE = 0.2
 
 FLOPS = 2 * F * M * N + 4 * M * N + 2 * R * M * N * N + 2 * R * H * N * N
@@ -27,30 +26,46 @@ def tile_mgatlayer_b_kernel(tc, x, w, att_self, att_neigh, b, adj_t, base, offs,
     with ExitStack() as ctx:
         held = ctx.enter_context(tc.tile_pool(name="held", bufs=1))
         head = ctx.enter_context(tc.tile_pool(name="head", bufs=2))
-        ring = ctx.enter_context(tc.tile_pool(name="ring", bufs=3))
+        ring = ctx.enter_context(tc.tile_pool(name="ring", bufs=4))
         prep = ctx.enter_context(tc.psum_pool(name="prep", bufs=2))
-        acc = ctx.enter_context(tc.psum_pool(name="acc", bufs=4))
-        turn = ctx.enter_context(tc.psum_pool(name="turn", bufs=2))
+        acc = ctx.enter_context(tc.psum_pool(name="acc", bufs=2 * R))
+        turn = ctx.enter_context(tc.psum_pool(name="turn", bufs=R))
 
-        offsets = held.tile([P, N // 16], U16, name="offsets")
-        nc.sync.dma_start(offsets[:], offs)
         att_rows = held.tile([P, P], BF16, name="att_rows")
         nc.vector.memset(att_rows[:], 0.0)
         nc.sync.dma_start(att_rows[0:H, :], att_self.rearrange("(h d) o -> h (d o)", d=P))
         nc.sync.dma_start(att_rows[H : 2 * H, :], att_neigh.rearrange("(h d) o -> h (d o)", d=P))
         w_sb = held.tile([P, FB, M], BF16, name="w_sb")
         x_sb = held.tile([P, FB, N], BF16, name="x_sb")
-        for k in range(FB):
-            nc.sync.dma_start(w_sb[:, k, :], w[k * P : (k + 1) * P, :])
-            nc.sync.dma_start(x_sb[:, k, :], x[k * P : (k + 1) * P, :])
-        b_rows = held.tile([P, M], F32, name="b_rows")
-        nc.sync.dma_start(b_rows[:], b.rearrange("m o -> (m o)").partition_broadcast(P))
-        adj = []
+        adj = [held.tile([P, R, N], BF16, name=f"adj{ub}") for ub in range(UB)]
+        w_blocks = w.rearrange("(k p) m -> p k m", p=P)
+
+        def load_x(jh):
+            for k in range(FB):
+                nc.sync.dma_start(x_sb[:, k, jh * W : (jh + 1) * W], x[k * P : (k + 1) * P, jh * W : (jh + 1) * W])
+
+        def load_adj(ub, jh):
+            nc.sync.dma_start(
+                adj[ub][:, :, jh * W : (jh + 1) * W],
+                adj_t[:, ub * P : (ub + 1) * P, jh * W : (jh + 1) * W].rearrange("r u j -> u r j"),
+            )
+
+        nc.sync.dma_start(w_sb[:, :, 0:P], w_blocks[:, :, 0:P])
+        load_x(0)
+        b_cols = held.tile([P, H], F32, name="b_cols")
+        nc.sync.dma_start(b_cols[:], b.rearrange("(h d) o -> d (h o)", d=P))
+        load_adj(0, 0)
+        load_adj(1, 0)
+        load_x(1)
+        load_adj(2, 0)
+        load_adj(3, 0)
+        nc.sync.dma_start(w_sb[:, :, P:M], w_blocks[:, :, P:M])
+        for ub in range(4, UB):
+            load_adj(ub, 0)
+        offsets = held.tile([P, N // 16], U16, name="offsets")
+        nc.sync.dma_start(offsets[:], offs)
         for ub in range(UB):
-            adj_ub = held.tile([P, R, N], BF16, name=f"adj{ub}")
-            for r in range(R):
-                nc.sync.dma_start(adj_ub[:, r, :], adj_t[r, ub * P : (ub + 1) * P, :])
-            adj.append(adj_ub)
+            load_adj(ub, 1)
         window = {}
         for h in range(H):
             for r in range(R):
@@ -62,9 +77,8 @@ def tile_mgatlayer_b_kernel(tc, x, w, att_self, att_neigh, b, adj_t, base, offs,
         ident_f32 = held.tile([P, P], F32, name="ident_f32")
         make_identity(nc, ident_bf[:])
         make_identity(nc, ident_f32[:])
-        feat_aug = [held.tile([P, UB, ROW], BF16, name=f"feat_aug{i}") for i in range(2)]
-        for i in range(2):
-            nc.gpsimd.memset(feat_aug[i][:, :, P:ROW], 1.0)
+        ones = held.tile([P, 16], BF16, name="ones")
+        nc.gpsimd.memset(ones[:], 1.0)
 
         att_ps = prep.tile([P, P], BF16, tag="prep", name="att_ps")
         nc.tensor.transpose(att_ps[:], att_rows[:], ident_bf[:])
@@ -73,124 +87,130 @@ def tile_mgatlayer_b_kernel(tc, x, w, att_self, att_neigh, b, adj_t, base, offs,
         att_self_rep = held.tile([P, H, P], BF16, name="att_self_rep")
         nc.vector.tensor_copy(att_self_rep[:], att_cols[:, 0:H].unsqueeze(2).to_broadcast([P, H, P]))
 
+        feat_b_t = [held.tile([P, UB, P], BF16, name=f"feat_b_t{h}") for h in range(H)]
+
         def prepare(h):
             feat = head.tile([P, N], BF16, name="feat")
-            feat_ps = [prep.tile([P, W], F32, tag="prep", name=f"feat_ps{jh}") for jh in range(JH)]
-            for k in range(FB):
-                for jh in range(JH):
+            feat_b = head.tile([P, N], BF16, name="feat_b")
+            s_row = head.tile([P, N], F32, name="s_row")
+            t_col = head.tile([P, UB], F32, name="t_col")
+            floor_col = head.tile([P, UB], F32, name="floor_col")
+            for jh in range(JH):
+                half = slice(jh * W, (jh + 1) * W)
+                blocks = slice(jh * QB, (jh + 1) * QB)
+                feat_ps = prep.tile([P, W], F32, tag="prep", name="feat_ps")
+                for k in range(FB):
                     nc.tensor.matmul(
-                        feat_ps[jh][:],
-                        w_sb[:, k, h * P : (h + 1) * P],
-                        x_sb[:, k, jh * W : (jh + 1) * W],
-                        start=(k == 0),
-                        stop=(k == FB - 1),
+                        feat_ps[:], w_sb[:, k, h * P : (h + 1) * P], x_sb[:, k, half], start=(k == 0), stop=(k == FB - 1)
                     )
-            for jh in range(JH):
-                nc.scalar.copy(feat[:, jh * W : (jh + 1) * W], feat_ps[jh][:])
+                nc.scalar.copy(feat[:, half], feat_ps[:])
+                nc.scalar.activation(feat_b[:, half], feat_ps[:], FN.Identity, bias=b_cols[:, h : h + 1])
 
-            s_steep = head.tile([P, N], F32, name="s_steep")
-            for jh in range(JH):
                 s_ps = prep.tile([P, W], F32, tag="prep", name="s_ps")
-                nc.tensor.matmul(s_ps[:], att_self_rep[:, h, :], feat[:, jh * W : (jh + 1) * W], start=True, stop=True)
-                nc.scalar.mul(s_steep[:, jh * W : (jh + 1) * W], s_ps[:], 1.0 - SLOPE)
-
-            t_ps = prep.tile([P, UB], F32, tag="prep", name="t_ps")
-            for ub in range(UB):
-                nc.tensor.matmul(
-                    t_ps[:, ub : ub + 1], feat[:, ub * P : (ub + 1) * P], att_cols[:, H + h : H + h + 1], start=True, stop=True
-                )
-            t_steep = head.tile([P, UB], F32, name="t_steep")
-            t_flat = head.tile([P, UB], F32, name="t_flat")
-            nc.vector.tensor_scalar_mul(t_steep[:], t_ps[:], 1.0 - SLOPE)
-            nc.vector.tensor_scalar_mul(t_flat[:], t_ps[:], SLOPE)
-
-            feat_t_ps = prep.tile([P, UB, P], BF16, tag="prep", name="feat_t_ps")
-            for ub in range(UB):
-                nc.tensor.transpose(feat_t_ps[:, ub, :], feat[:, ub * P : (ub + 1) * P], ident_bf[:])
-            nc.vector.tensor_copy(feat_aug[h % 2][:, :, 0:P], feat_t_ps[:])
-            return t_steep, t_flat, s_steep
-
-        def attention(jh, prepared, relu_on_vector):
-            t_steep, t_flat, s_steep = prepared
-            p_blocks = []
-            for ub in range(UB):
-                steep = ring.tile([P, W], F32, name="steep")
-                if relu_on_vector:
-                    nc.vector.tensor_scalar(
-                        steep[:], s_steep[:, jh * W : (jh + 1) * W], t_steep[:, ub : ub + 1], 0.0, op0=ALU.add, op1=ALU.max
-                    )
-                else:
-                    nc.scalar.activation(steep[:], s_steep[:, jh * W : (jh + 1) * W], FN.Relu, bias=t_steep[:, ub : ub + 1])
-                e = ring.tile([P, W], BF16, name="e", bufs=4)
-                nc.scalar.activation(e[:], steep[:], FN.Exp, bias=t_flat[:, ub : ub + 1], scale=1.0)
-                p = ring.tile([P, R, W], BF16, name="p", bufs=2 * UB)
-                nc.vector.tensor_tensor(
-                    p[:], e[:].unsqueeze(1).to_broadcast([P, R, W]), adj[ub][:, :, jh * W : (jh + 1) * W], ALU.mult
-                )
-                p_blocks.append(p)
-            return p_blocks
-
-        def sums_over_neighbours(h, r, p_blocks):
-            sums = [acc.tile([P, PAIR, P + 1], F32, tag="acc", name=f"sums{i}") for i in range(QB // PAIR)]
-            for q in range(QB):
-                for ub in range(UB):
+                nc.tensor.matmul(s_ps[:], att_self_rep[:, h, :], feat[:, half], start=True, stop=True)
+                t_ps = prep.tile([P, QB], F32, tag="prep", name="t_ps")
+                for i in range(QB):
+                    ub = jh * QB + i
                     nc.tensor.matmul(
-                        sums[q // PAIR][:, q % PAIR, :],
-                        p_blocks[ub][:, r, q * P : (q + 1) * P],
-                        feat_aug[h % 2][:, ub, 0 : P + 1],
-                        start=(ub == 0),
-                        stop=(ub == UB - 1),
+                        t_ps[:, i : i + 1], feat[:, ub * P : (ub + 1) * P], att_cols[:, H + h : H + h + 1], start=True, stop=True
                     )
-            return sums
+                nc.scalar.mul(s_row[:, half], s_ps[:], 1.0 - SLOPE)
+                nc.scalar.copy(t_col[:, blocks], t_ps[:])
+                nc.scalar.activation(floor_col[:, blocks], t_ps[:], FN.Exp, scale=SLOPE)
 
-        def begin_placing(h, sums):
-            inv_cols = ring.tile([P, QB], F32, name="inv_cols")
-            biased_t = ring.tile([P, QB, P], F32, name="biased_t")
-            for i in range(QB // PAIR):
-                nc.vector.reciprocal(inv_cols[:, i * PAIR : (i + 1) * PAIR], sums[i][:, :, P])
-            for q in range(QB):
-                nc.vector.scalar_tensor_tensor(
-                    biased_t[:, q, :],
-                    b_rows[:, h * P : (h + 1) * P],
-                    sums[q // PAIR][:, q % PAIR, P : P + 1],
-                    sums[q // PAIR][:, q % PAIR, 0:P],
-                    op0=ALU.mult,
-                    op1=ALU.add,
+                feat_t_ps = prep.tile([P, QB, P], BF16, tag="prep", name="feat_t_ps")
+                for i in range(QB):
+                    ub = jh * QB + i
+                    nc.tensor.transpose(feat_t_ps[:, i, :], feat_b[:, ub * P : (ub + 1) * P], ident_bf[:])
+                nc.vector.tensor_copy(feat_b_t[h][:, blocks, :], feat_t_ps[:])
+            return s_row, t_col, floor_col
+
+        def weigh(k, ub):
+            s_row, t_col, floor_col = prepared[k // JH]
+            jh = k % JH
+            steep = ring.tile([P, W], BF16, name="steep", bufs=UB)
+            nc.scalar.activation(steep[:], s_row[:, jh * W : (jh + 1) * W], FN.Exp, bias=t_col[:, ub : ub + 1])
+            e = ring.tile([P, W], BF16, name="e")
+            nc.vector.tensor_scalar_max(e[:], steep[:], floor_col[:, ub : ub + 1])
+            return e
+
+        def mask(k, ub, e):
+            jh = k % JH
+            p = ring.tile([P, R, W], BF16, name="p", bufs=2 * UB)
+            nc.vector.tensor_tensor(
+                p[:], e[:].unsqueeze(1).to_broadcast([P, R, W]), adj[ub][:, :, jh * W : (jh + 1) * W], ALU.mult
+            )
+            return p
+
+        def add_block(k, ub, p, biased_ps):
+            for r in range(R):
+                nc.tensor.matmul(
+                    biased_ps[r][:], feat_b_t[k // JH][:, ub, :], p[:, r, :], start=(ub == 0), stop=(ub == UB - 1)
                 )
-            return biased_t, inv_cols
 
-        def finish_placing(h, jh, r, biased_t, inv_cols):
-            biased_ps = turn.tile([P, W], F32, tag="turn", name="biased_ps")
-            for q in range(QB):
-                nc.tensor.transpose(biased_ps[:, q * P : (q + 1) * P], biased_t[:, q, :], ident_f32[:])
-            positive = ring.tile([P, W], F32, name="positive")
-            nc.scalar.activation(positive[:], biased_ps[:], FN.Relu)
-            inv_ps = turn.tile([P, W], F32, tag="turn", name="inv_ps")
+        def sum_den(p_blocks):
+            den_ps = prep.tile([P, R, QB], F32, tag="prep", name="den_ps")
+            for r in range(R):
+                for q in range(QB):
+                    for ub in range(UB):
+                        nc.tensor.matmul(
+                            den_ps[:, r, q : q + 1],
+                            p_blocks[ub][:, r, q * P : (q + 1) * P],
+                            ones[:, 0:1],
+                            start=(ub == 0),
+                            stop=(ub == UB - 1),
+                        )
+            return den_ps
+
+        def spread_inverse(inv_cols, r):
+            inv_ps = turn.tile([P, W], F32, name="inv_ps")
             for q in range(QB):
                 nc.tensor.transpose(
-                    inv_ps[:, q * P : (q + 1) * P], inv_cols[:, q : q + 1].to_broadcast([P, P]), ident_f32[:]
+                    inv_ps[:, q * P : (q + 1) * P], inv_cols[:, r, q : q + 1].to_broadcast([P, P]), ident_f32[:]
                 )
-            inv_den = ring.tile([P, W], F32, name="inv_den")
-            nc.scalar.copy(inv_den[:], inv_ps[:])
+            return inv_ps
+
+        def scatter(k, r, positive, inv_den):
+            h, jh = divmod(k, JH)
             piece = offsets[:, jh * (W // 16) : (jh + 1) * (W // 16)]
             nc.vector.tensor_tensor(window[r, h][:].indirect(piece), positive[:], inv_den[:], ALU.mult)
             if jh == JH - 1:
                 row = r * M + h * P
                 nc.sync.dma_start(out[row : row + P, :], window[r, h][:])
 
-        prepared = prepare(0)
-        half_placed = None
-        for h in range(H):
-            for jh in range(JH):
-                p_blocks = attention(jh, prepared, relu_on_vector=(h == 0 and jh == 0))
-                for r in range(R):
-                    if jh == 0 and r == 1 and h + 1 < H:
-                        upcoming = prepare(h + 1)
-                    sums = sums_over_neighbours(h, r, p_blocks)
-                    biased_t, inv_cols = begin_placing(h, sums)
-                    if half_placed is not None:
-                        finish_placing(*half_placed)
-                    half_placed = (h, jh, r, biased_t, inv_cols)
-            if h + 1 < H:
-                prepared = upcoming
-        finish_placing(*half_placed)
+        prepared = {0: prepare(0)}
+        biased, den = {}, {}
+
+        def place(k, r):
+            inv_den = ring.tile([P, W], F32, name="inv_den")
+            nc.scalar.copy(inv_den[:], inv_ps[r][:])
+            scatter(k, r, positive[r], inv_den)
+
+        e_next = weigh(0, 0)
+        for k in range(PASSES + 1):
+            p_blocks = []
+            for ub in range(UB):
+                if k < PASSES:
+                    if ub == 0:
+                        biased[k] = [acc.tile([P, W], F32, tag="acc", name=f"biased_ps{r}") for r in range(R)]
+                    e = e_next
+                    if k * UB + ub + 1 < PASSES * UB:
+                        e_next = weigh(*divmod(k * UB + ub + 1, UB))
+                    p_blocks.append(mask(k, ub, e))
+                    add_block(k, ub, p_blocks[ub], biased[k])
+                if k > 0 and ub == 0:
+                    inv_cols = ring.tile([P, R, QB], F32, name="inv_cols")
+                    nc.vector.reciprocal(inv_cols[:], den[k - 1][:])
+                    inv_ps = [spread_inverse(inv_cols, r) for r in range(R)]
+                if k > 0 and ub == 1:
+                    positive = [ring.tile([P, W], F32, name=f"positive{r}") for r in range(R)]
+                    for r in range(R):
+                        nc.scalar.activation(positive[r][:], biased[k - 1][r][:], FN.Relu)
+                if k > 0 and ub == UB // 2 - 1:
+                    place(k - 1, 0)
+                if k > 0 and ub == UB - 1:
+                    place(k - 1, 1)
+            if k < PASSES:
+                den[k] = sum_den(p_blocks)
+            if k % JH == 0 and k // JH + 1 < H:
+                prepared[k // JH + 1] = prepare(k // JH + 1)

@@ -16,6 +16,7 @@ W = 512
 JH = N // W
 QB = W // P
 PASSES = H * JH
+AHEAD = UB
 SLOPE = 0.2
 
 FLOPS = 2 * F * M * N + 4 * M * N + 2 * R * M * N * N + 2 * R * H * N * N
@@ -27,8 +28,8 @@ def tile_mgatlayer_b_kernel(tc, x, w, att_self, att_neigh, b, adj_t, base, offs,
         held = ctx.enter_context(tc.tile_pool(name="held", bufs=1))
         head = ctx.enter_context(tc.tile_pool(name="head", bufs=2))
         ring = ctx.enter_context(tc.tile_pool(name="ring", bufs=4))
-        prep = ctx.enter_context(tc.psum_pool(name="prep", bufs=2))
-        acc = ctx.enter_context(tc.psum_pool(name="acc", bufs=2 * R))
+        prep = ctx.enter_context(tc.psum_pool(name="prep", bufs=4))
+        acc = ctx.enter_context(tc.psum_pool(name="acc", bufs=R))
         turn = ctx.enter_context(tc.psum_pool(name="turn", bufs=R))
 
         att_rows = held.tile([P, P], BF16, name="att_rows")
@@ -122,14 +123,21 @@ def tile_mgatlayer_b_kernel(tc, x, w, att_self, att_neigh, b, adj_t, base, offs,
                 for i in range(QB):
                     ub = jh * QB + i
                     nc.tensor.transpose(feat_t_ps[:, i, :], feat_b[:, ub * P : (ub + 1) * P], ident_bf[:])
-                nc.vector.tensor_copy(feat_b_t[h][:, blocks, :], feat_t_ps[:])
+                if h == 0:
+                    nc.vector.tensor_copy(feat_b_t[h][:, blocks, :], feat_t_ps[:])
+                else:
+                    nc.scalar.copy(feat_b_t[h][:, blocks, :], feat_t_ps[:])
             return s_row, t_col, floor_col
 
-        def weigh(k, ub):
+        def exponential(k, ub):
             s_row, t_col, floor_col = prepared[k // JH]
             jh = k % JH
-            steep = ring.tile([P, W], BF16, name="steep", bufs=UB)
+            steep = ring.tile([P, W], BF16, name="steep", bufs=AHEAD + 2)
             nc.scalar.activation(steep[:], s_row[:, jh * W : (jh + 1) * W], FN.Exp, bias=t_col[:, ub : ub + 1])
+            return steep
+
+        def maximum(k, ub, steep):
+            s_row, t_col, floor_col = prepared[k // JH]
             e = ring.tile([P, W], BF16, name="e")
             nc.vector.tensor_scalar_max(e[:], steep[:], floor_col[:, ub : ub + 1])
             return e
@@ -178,39 +186,45 @@ def tile_mgatlayer_b_kernel(tc, x, w, att_self, att_neigh, b, adj_t, base, offs,
                 row = r * M + h * P
                 nc.sync.dma_start(out[row : row + P, :], window[r, h][:])
 
+        BLOCKS = PASSES * UB
         prepared = {0: prepare(0)}
-        biased, den = {}, {}
+        steep = {g: exponential(*divmod(g, UB)) for g in range(AHEAD)}
+        e = {0: maximum(0, 0, steep[0])}
+        positive, inv_ps, inv_den = {}, {}, {}
 
-        def place(k, r):
-            inv_den = ring.tile([P, W], F32, name="inv_den")
-            nc.scalar.copy(inv_den[:], inv_ps[r][:])
-            scatter(k, r, positive[r], inv_den)
+        def copy_inverse(k, r):
+            inv_den[k, r] = ring.tile([P, W], F32, name=f"inv_den{r}")
+            nc.scalar.copy(inv_den[k, r][:], inv_ps[k, r][:])
 
-        e_next = weigh(0, 0)
         for k in range(PASSES + 1):
-            p_blocks = []
-            for ub in range(UB):
-                if k < PASSES:
-                    if ub == 0:
-                        biased[k] = [acc.tile([P, W], F32, tag="acc", name=f"biased_ps{r}") for r in range(R)]
-                    e = e_next
-                    if k * UB + ub + 1 < PASSES * UB:
-                        e_next = weigh(*divmod(k * UB + ub + 1, UB))
-                    p_blocks.append(mask(k, ub, e))
-                    add_block(k, ub, p_blocks[ub], biased[k])
-                if k > 0 and ub == 0:
-                    inv_cols = ring.tile([P, R, QB], F32, name="inv_cols")
-                    nc.vector.reciprocal(inv_cols[:], den[k - 1][:])
-                    inv_ps = [spread_inverse(inv_cols, r) for r in range(R)]
-                if k > 0 and ub == 1:
-                    positive = [ring.tile([P, W], F32, name=f"positive{r}") for r in range(R)]
-                    for r in range(R):
-                        nc.scalar.activation(positive[r][:], biased[k - 1][r][:], FN.Relu)
-                if k > 0 and ub == UB // 2 - 1:
-                    place(k - 1, 0)
-                if k > 0 and ub == UB - 1:
-                    place(k - 1, 1)
             if k < PASSES:
-                den[k] = sum_den(p_blocks)
-            if k % JH == 0 and k // JH + 1 < H:
-                prepared[k // JH + 1] = prepare(k // JH + 1)
+                biased_ps = [acc.tile([P, W], F32, tag="acc", name=f"biased_ps{r}") for r in range(R)]
+                p_blocks = []
+                for ub in range(UB):
+                    g = k * UB + ub
+                    if g + AHEAD < BLOCKS:
+                        if (g + AHEAD) % (JH * UB) == 0:
+                            prepared[(g + AHEAD) // (JH * UB)] = prepare((g + AHEAD) // (JH * UB))
+                        steep[g + AHEAD] = exponential(*divmod(g + AHEAD, UB))
+                    if g + 1 < BLOCKS:
+                        e[g + 1] = maximum(*divmod(g + 1, UB), steep[g + 1])
+                    p_blocks.append(mask(k, ub, e[g]))
+                    add_block(k, ub, p_blocks[ub], biased_ps)
+                den_ps = sum_den(p_blocks)
+            if k > 0:
+                scatter(k - 1, 0, positive[k - 1, 0], inv_den[k - 1, 0])
+            if k < PASSES:
+                for r in range(R):
+                    positive[k, r] = ring.tile([P, W], F32, name=f"positive{r}")
+                    nc.scalar.activation(positive[k, r][:], biased_ps[r][:], FN.Relu)
+                inv_cols = ring.tile([P, R, QB], F32, name="inv_cols")
+                nc.vector.reciprocal(inv_cols[:], den_ps[:])
+                inv_ps[k, 0] = spread_inverse(inv_cols, 0)
+            if k > 0:
+                copy_inverse(k - 1, 1)
+            if k < PASSES:
+                inv_ps[k, 1] = spread_inverse(inv_cols, 1)
+            if k > 0:
+                scatter(k - 1, 1, positive[k - 1, 1], inv_den[k - 1, 1])
+            if k < PASSES:
+                copy_inverse(k, 0)

@@ -55,13 +55,11 @@ def tile_mgatlayer_b_kernel(tc, x, w, att_self, att_neigh, b, adj_t, base, offs,
         load_x(0)
         b_cols = held.tile([P, H], F32, name="b_cols")
         nc.sync.dma_start(b_cols[:], b.rearrange("(h d) o -> d (h o)", d=P))
-        load_adj(0, 0)
-        load_adj(1, 0)
         load_x(1)
-        load_adj(2, 0)
-        load_adj(3, 0)
+        for ub in range(UB // 2):
+            load_adj(ub, 0)
         nc.sync.dma_start(w_sb[:, :, P:M], w_blocks[:, :, P:M])
-        for ub in range(4, UB):
+        for ub in range(UB // 2, UB):
             load_adj(ub, 0)
         offsets = held.tile([P, N // 16], U16, name="offsets")
         nc.sync.dma_start(offsets[:], offs)
@@ -105,7 +103,10 @@ def tile_mgatlayer_b_kernel(tc, x, w, att_self, att_neigh, b, adj_t, base, offs,
                         feat_ps[:], w_sb[:, k, h * P : (h + 1) * P], x_sb[:, k, half], start=(k == 0), stop=(k == FB - 1)
                     )
                 nc.scalar.copy(feat[:, half], feat_ps[:])
-                nc.scalar.activation(feat_b[:, half], feat_ps[:], FN.Identity, bias=b_cols[:, h : h + 1])
+                if h == 0:
+                    nc.vector.tensor_scalar_add(feat_b[:, half], feat_ps[:], b_cols[:, h : h + 1])
+                else:
+                    nc.scalar.activation(feat_b[:, half], feat_ps[:], FN.Identity, bias=b_cols[:, h : h + 1])
 
                 s_ps = prep.tile([P, W], F32, tag="prep", name="s_ps")
                 nc.tensor.matmul(s_ps[:], att_self_rep[:, h, :], feat[:, half], start=True, stop=True)

@@ -17,6 +17,7 @@ JH = N // W
 QB = W // P
 PASSES = H * JH
 AHEAD = UB
+PAIR = 2
 SLOPE = 0.2
 
 FLOPS = 2 * F * M * N + 4 * M * N + 2 * R * M * N * N + 2 * R * H * N * N
@@ -38,7 +39,7 @@ def tile_mgatlayer_b_kernel(tc, x, w, att_self, att_neigh, b, adj_t, base, offs,
         nc.sync.dma_start(att_rows[H : 2 * H, :], att_neigh.rearrange("(h d) o -> h (d o)", d=P))
         w_sb = held.tile([P, FB, M], BF16, name="w_sb")
         x_sb = held.tile([P, FB, N], BF16, name="x_sb")
-        adj = [held.tile([P, R, N], BF16, name=f"adj{ub}") for ub in range(UB)]
+        adj = [held.tile([P, PAIR, R, N], BF16, name=f"adj{i}") for i in range(UB // PAIR)]
         w_blocks = w.rearrange("(k p) m -> p k m", p=P)
 
         def load_x(jh):
@@ -47,7 +48,7 @@ def tile_mgatlayer_b_kernel(tc, x, w, att_self, att_neigh, b, adj_t, base, offs,
 
         def load_adj(ub, jh):
             nc.sync.dma_start(
-                adj[ub][:, :, jh * W : (jh + 1) * W],
+                adj[ub // PAIR][:, ub % PAIR, :, jh * W : (jh + 1) * W],
                 adj_t[:, ub * P : (ub + 1) * P, jh * W : (jh + 1) * W].rearrange("r u j -> u r j"),
             )
 
@@ -137,34 +138,40 @@ def tile_mgatlayer_b_kernel(tc, x, w, att_self, att_neigh, b, adj_t, base, offs,
             nc.scalar.activation(steep[:], s_row[:, jh * W : (jh + 1) * W], FN.Exp, bias=t_col[:, ub : ub + 1])
             return steep
 
-        def maximum(k, ub, steep):
+        def maxima(k, i):
             s_row, t_col, floor_col = prepared[k // JH]
-            e = ring.tile([P, W], BF16, name="e")
-            nc.vector.tensor_scalar_max(e[:], steep[:], floor_col[:, ub : ub + 1])
+            e = ring.tile([P, PAIR, W], BF16, name="e")
+            for c in range(PAIR):
+                ub = i * PAIR + c
+                nc.vector.tensor_scalar_max(e[:, c, :], steep[k * UB + ub][:], floor_col[:, ub : ub + 1])
             return e
 
-        def mask(k, ub, e):
+        def mask(k, i, e):
             jh = k % JH
-            p = ring.tile([P, R, W], BF16, name="p", bufs=2 * UB)
+            p = ring.tile([P, PAIR, R, W], BF16, name="p", bufs=2 * UB // PAIR)
             nc.vector.tensor_tensor(
-                p[:], e[:].unsqueeze(1).to_broadcast([P, R, W]), adj[ub][:, :, jh * W : (jh + 1) * W], ALU.mult
+                p[:], e[:].unsqueeze(2).to_broadcast([P, PAIR, R, W]), adj[i][:, :, :, jh * W : (jh + 1) * W], ALU.mult
             )
             return p
 
         def add_block(k, ub, p, biased_ps):
             for r in range(R):
                 nc.tensor.matmul(
-                    biased_ps[r][:], feat_b_t[k // JH][:, ub, :], p[:, r, :], start=(ub == 0), stop=(ub == UB - 1)
+                    biased_ps[r][:],
+                    feat_b_t[k // JH][:, ub, :],
+                    p[:, ub % PAIR, r, :],
+                    start=(ub == 0),
+                    stop=(ub == UB - 1),
                 )
 
-        def sum_den(p_blocks):
+        def sum_den(p_pairs):
             den_ps = prep.tile([P, R, QB], F32, tag="prep", name="den_ps")
             for r in range(R):
                 for q in range(QB):
                     for ub in range(UB):
                         nc.tensor.matmul(
                             den_ps[:, r, q : q + 1],
-                            p_blocks[ub][:, r, q * P : (q + 1) * P],
+                            p_pairs[ub // PAIR][:, ub % PAIR, r, q * P : (q + 1) * P],
                             ones[:, 0:1],
                             start=(ub == 0),
                             stop=(ub == UB - 1),
@@ -190,7 +197,7 @@ def tile_mgatlayer_b_kernel(tc, x, w, att_self, att_neigh, b, adj_t, base, offs,
         BLOCKS = PASSES * UB
         prepared = {0: prepare(0)}
         steep = {g: exponential(*divmod(g, UB)) for g in range(AHEAD)}
-        e = {0: maximum(0, 0, steep[0])}
+        e_next = maxima(0, 0)
         positive, inv_ps, inv_den = {}, {}, {}
 
         def copy_inverse(k, r):
@@ -200,18 +207,20 @@ def tile_mgatlayer_b_kernel(tc, x, w, att_self, att_neigh, b, adj_t, base, offs,
         for k in range(PASSES + 1):
             if k < PASSES:
                 biased_ps = [acc.tile([P, W], F32, tag="acc", name=f"biased_ps{r}") for r in range(R)]
-                p_blocks = []
-                for ub in range(UB):
-                    g = k * UB + ub
-                    if g + AHEAD < BLOCKS:
-                        if (g + AHEAD) % (JH * UB) == 0:
-                            prepared[(g + AHEAD) // (JH * UB)] = prepare((g + AHEAD) // (JH * UB))
-                        steep[g + AHEAD] = exponential(*divmod(g + AHEAD, UB))
-                    if g + 1 < BLOCKS:
-                        e[g + 1] = maximum(*divmod(g + 1, UB), steep[g + 1])
-                    p_blocks.append(mask(k, ub, e[g]))
-                    add_block(k, ub, p_blocks[ub], biased_ps)
-                den_ps = sum_den(p_blocks)
+                p_pairs = []
+                for i in range(UB // PAIR):
+                    for g in range(k * UB + i * PAIR, k * UB + (i + 1) * PAIR):
+                        if g + AHEAD < BLOCKS:
+                            if (g + AHEAD) % (JH * UB) == 0:
+                                prepared[(g + AHEAD) // (JH * UB)] = prepare((g + AHEAD) // (JH * UB))
+                            steep[g + AHEAD] = exponential(*divmod(g + AHEAD, UB))
+                    e = e_next
+                    if k * UB + (i + 1) * PAIR < BLOCKS:
+                        e_next = maxima(*divmod(k * (UB // PAIR) + i + 1, UB // PAIR))
+                    p_pairs.append(mask(k, i, e))
+                    for ub in range(i * PAIR, (i + 1) * PAIR):
+                        add_block(k, ub, p_pairs[i], biased_ps)
+                den_ps = sum_den(p_pairs)
             if k > 0:
                 scatter(k - 1, 0, positive[k - 1, 0], inv_den[k - 1, 0])
             if k < PASSES:

@@ -89,57 +89,61 @@ def tile_mgatlayer_b_kernel(tc, x, w, att_self, att_neigh, b, adj_t, base, offs,
 
         feat_b_t = [held.tile([P, UB, P], BF16, name=f"feat_b_t{h}") for h in range(H)]
 
-        def prepare(h):
+        def new_head():
             feat = head.tile([P, N], BF16, name="feat")
             feat_b = head.tile([P, N], BF16, name="feat_b")
             s_row = head.tile([P, N], F32, name="s_row")
             t_col = head.tile([P, UB], F32, name="t_col")
             floor_col = head.tile([P, UB], F32, name="floor_col")
-            for jh in range(JH):
-                half = slice(jh * W, (jh + 1) * W)
-                blocks = slice(jh * QB, (jh + 1) * QB)
-                feat_ps = prep.tile([P, W], F32, tag="prep", name="feat_ps")
-                for k in range(FB):
-                    nc.tensor.matmul(
-                        feat_ps[:], w_sb[:, k, h * P : (h + 1) * P], x_sb[:, k, half], start=(k == 0), stop=(k == FB - 1)
-                    )
-                nc.scalar.copy(feat[:, half], feat_ps[:])
-                if h == 0:
-                    nc.vector.tensor_scalar_add(feat_b[:, half], feat_ps[:], b_cols[:, h : h + 1])
-                else:
-                    nc.scalar.activation(feat_b[:, half], feat_ps[:], FN.Identity, bias=b_cols[:, h : h + 1])
+            return s_row, t_col, floor_col, feat, feat_b
 
-                s_ps = prep.tile([P, W], F32, tag="prep", name="s_ps")
-                nc.tensor.matmul(s_ps[:], att_self_rep[:, h, :], feat[:, half], start=True, stop=True)
-                t_ps = prep.tile([P, QB], F32, tag="prep", name="t_ps")
-                for i in range(QB):
-                    ub = jh * QB + i
-                    nc.tensor.matmul(
-                        t_ps[:, i : i + 1], feat[:, ub * P : (ub + 1) * P], att_cols[:, H + h : H + h + 1], start=True, stop=True
-                    )
-                nc.scalar.mul(s_row[:, half], s_ps[:], 1.0 - SLOPE)
-                nc.scalar.copy(t_col[:, blocks], t_ps[:])
-                nc.scalar.activation(floor_col[:, blocks], t_ps[:], FN.Exp, scale=SLOPE)
+        def prepare_scores(h, jh):
+            s_row, t_col, floor_col, feat, feat_b = prepared[h]
+            half = slice(jh * W, (jh + 1) * W)
+            blocks = slice(jh * QB, (jh + 1) * QB)
+            feat_ps = prep.tile([P, W], F32, tag="prep", name="feat_ps")
+            for k in range(FB):
+                nc.tensor.matmul(
+                    feat_ps[:], w_sb[:, k, h * P : (h + 1) * P], x_sb[:, k, half], start=(k == 0), stop=(k == FB - 1)
+                )
+            nc.scalar.copy(feat[:, half], feat_ps[:])
+            if h == 0:
+                nc.vector.tensor_scalar_add(feat_b[:, half], feat_ps[:], b_cols[:, h : h + 1])
+            else:
+                nc.scalar.activation(feat_b[:, half], feat_ps[:], FN.Identity, bias=b_cols[:, h : h + 1])
+            s_ps = prep.tile([P, W], F32, tag="prep", name="s_ps")
+            nc.tensor.matmul(s_ps[:], att_self_rep[:, h, :], feat[:, half], start=True, stop=True)
+            t_ps = prep.tile([P, QB], F32, tag="prep", name="t_ps")
+            for i in range(QB):
+                ub = jh * QB + i
+                nc.tensor.matmul(
+                    t_ps[:, i : i + 1], feat[:, ub * P : (ub + 1) * P], att_cols[:, H + h : H + h + 1], start=True, stop=True
+                )
+            nc.scalar.mul(s_row[:, half], s_ps[:], 1.0 - SLOPE)
+            nc.scalar.copy(t_col[:, blocks], t_ps[:])
+            nc.scalar.activation(floor_col[:, blocks], t_ps[:], FN.Exp, scale=SLOPE)
 
-                feat_t_ps = prep.tile([P, QB, P], BF16, tag="prep", name="feat_t_ps")
-                for i in range(QB):
-                    ub = jh * QB + i
-                    nc.tensor.transpose(feat_t_ps[:, i, :], feat_b[:, ub * P : (ub + 1) * P], ident_bf[:])
-                if h == 0:
-                    nc.vector.tensor_copy(feat_b_t[h][:, blocks, :], feat_t_ps[:])
-                else:
-                    nc.scalar.copy(feat_b_t[h][:, blocks, :], feat_t_ps[:])
-            return s_row, t_col, floor_col
+        def prepare_operand(h, jh):
+            feat_b = prepared[h][4]
+            blocks = slice(jh * QB, (jh + 1) * QB)
+            feat_t_ps = prep.tile([P, QB, P], BF16, tag="prep", name="feat_t_ps")
+            for i in range(QB):
+                ub = jh * QB + i
+                nc.tensor.transpose(feat_t_ps[:, i, :], feat_b[:, ub * P : (ub + 1) * P], ident_bf[:])
+            if h == 0:
+                nc.vector.tensor_copy(feat_b_t[h][:, blocks, :], feat_t_ps[:])
+            else:
+                nc.scalar.copy(feat_b_t[h][:, blocks, :], feat_t_ps[:])
 
         def exponential(k, ub):
-            s_row, t_col, floor_col = prepared[k // JH]
+            s_row, t_col = prepared[k // JH][0:2]
             jh = k % JH
             steep = ring.tile([P, W], BF16, name="steep", bufs=AHEAD + 2)
             nc.scalar.activation(steep[:], s_row[:, jh * W : (jh + 1) * W], FN.Exp, bias=t_col[:, ub : ub + 1])
             return steep
 
         def maxima(k, i):
-            s_row, t_col, floor_col = prepared[k // JH]
+            floor_col = prepared[k // JH][2]
             e = ring.tile([P, PAIR, W], BF16, name="e")
             for c in range(PAIR):
                 ub = i * PAIR + c
@@ -195,7 +199,10 @@ def tile_mgatlayer_b_kernel(tc, x, w, att_self, att_neigh, b, adj_t, base, offs,
                 nc.sync.dma_start(out[row : row + P, :], window[r, h][:])
 
         BLOCKS = PASSES * UB
-        prepared = {0: prepare(0)}
+        prepared = {0: new_head()}
+        for jh in range(JH):
+            prepare_scores(0, jh)
+            prepare_operand(0, jh)
         steep = {g: exponential(*divmod(g, UB)) for g in range(AHEAD)}
         e_next = maxima(0, 0)
         positive, inv_ps, inv_den = {}, {}, {}
@@ -212,8 +219,13 @@ def tile_mgatlayer_b_kernel(tc, x, w, att_self, att_neigh, b, adj_t, base, offs,
                     for g in range(k * UB + i * PAIR, k * UB + (i + 1) * PAIR):
                         if g + AHEAD < BLOCKS:
                             if (g + AHEAD) % (JH * UB) == 0:
-                                prepared[(g + AHEAD) // (JH * UB)] = prepare((g + AHEAD) // (JH * UB))
+                                prepared[(g + AHEAD) // (JH * UB)] = new_head()
+                                for jh in range(JH):
+                                    prepare_scores((g + AHEAD) // (JH * UB), jh)
                             steep[g + AHEAD] = exponential(*divmod(g + AHEAD, UB))
+                            if (g + AHEAD) % (JH * UB) == 0:
+                                for jh in range(JH):
+                                    prepare_operand((g + AHEAD) // (JH * UB), jh)
                     e = e_next
                     if k * UB + (i + 1) * PAIR < BLOCKS:
                         e_next = maxima(*divmod(k * (UB // PAIR) + i + 1, UB // PAIR))

@@ -240,7 +240,12 @@ def tile_mgatlayer_b_kernel(tc, x, w, att_self, att_neigh, b, adj_t, base, offs,
                     positive[k, r] = ring.tile([P, W], F32, name=f"positive{r}")
                     nc.scalar.activation(positive[k, r][:], biased_ps[r][:], FN.Relu)
                 inv_cols = ring.tile([P, R, QB], F32, name="inv_cols")
-                nc.vector.reciprocal(inv_cols[:], den_ps[:])
+                if k < PASSES - 1:
+                    nc.vector.reciprocal(inv_cols[:], den_ps[:])
+                else:
+                    inv_root = ring.tile([P, R, QB], F32, name="inv_root")
+                    nc.scalar.activation(inv_root[:], den_ps[:], FN.Abs_reciprocal_sqrt)
+                    nc.scalar.activation(inv_cols[:], inv_root[:], FN.Square)
                 inv_ps[k, 0] = spread_inverse(inv_cols, 0)
             if k > 0:
                 copy_inverse(k - 1, 1)

@@ -16,9 +16,12 @@ W = 512
 JH = N // W
 QB = W // P
 PASSES = H * JH
-AHEAD = UB
 PAIR = 2
+PAIRS = UB // PAIR
+AHEAD = PAIRS
+LAST_EXP = (H - 1) * JH - 1
 SLOPE = 0.2
+HUGE = 2.0**100
 
 FLOPS = 2 * F * M * N + 4 * M * N + 2 * R * M * N * N + 2 * R * H * N * N
 
@@ -56,8 +59,10 @@ def tile_mgatlayer_b_kernel(tc, x, w, att_self, att_neigh, b, adj_t, base, offs,
         load_x(0)
         b_cols = held.tile([P, H], F32, name="b_cols")
         nc.sync.dma_start(b_cols[:], b.rearrange("(h d) o -> d (h o)", d=P))
+        for ub in range(PAIR):
+            load_adj(ub, 0)
         load_x(1)
-        for ub in range(UB // 2):
+        for ub in range(PAIR, UB // 2):
             load_adj(ub, 0)
         nc.sync.dma_start(w_sb[:, :, P:M], w_blocks[:, :, P:M])
         for ub in range(UB // 2, UB):
@@ -77,28 +82,32 @@ def tile_mgatlayer_b_kernel(tc, x, w, att_self, att_neigh, b, adj_t, base, offs,
         ident_f32 = held.tile([P, P], F32, name="ident_f32")
         make_identity(nc, ident_bf[:])
         make_identity(nc, ident_f32[:])
-        ones = held.tile([P, 16], BF16, name="ones")
+        ones = held.tile([P, P], BF16, name="ones")
         nc.gpsimd.memset(ones[:], 1.0)
+        minus_one = held.tile([P, 1], F32, name="minus_one")
+        nc.gpsimd.memset(minus_one[:], -1.0)
 
         att_ps = prep.tile([P, P], BF16, tag="prep", name="att_ps")
         nc.tensor.transpose(att_ps[:], att_rows[:], ident_bf[:])
         att_cols = held.tile([P, 2 * H], BF16, name="att_cols")
-        nc.vector.tensor_copy(att_cols[:], att_ps[:, 0 : 2 * H])
+        nc.scalar.copy(att_cols[:], att_ps[:, 0 : 2 * H])
         att_self_rep = held.tile([P, H, P], BF16, name="att_self_rep")
         nc.vector.tensor_copy(att_self_rep[:], att_cols[:, 0:H].unsqueeze(2).to_broadcast([P, H, P]))
 
-        feat_b_t = [held.tile([P, UB, P], BF16, name=f"feat_b_t{h}") for h in range(H)]
+        feat_b_g = [held.tile([P, UB, P], BF16, name=f"feat_b_g{h}") for h in range(H)]
 
         def new_head():
             feat = head.tile([P, N], BF16, name="feat")
-            feat_b = head.tile([P, N], BF16, name="feat_b")
-            s_row = head.tile([P, N], F32, name="s_row")
-            t_col = head.tile([P, UB], F32, name="t_col")
-            floor_col = head.tile([P, UB], F32, name="floor_col")
-            return s_row, t_col, floor_col, feat, feat_b
+            feat_b = head.tile([P, N], F32, name="feat_b")
+            c_row = head.tile([P, N], F32, name="c_row")
+            a_col = head.tile([P, UB], F32, name="a_col")
+            g_bf = head.tile([P, UB], BF16, name="g_bf")
+            g_col = head.tile([P, UB], F32, name="g_col")
+            constant = head.tile([P, 1], F32, name="constant")
+            return feat, feat_b, c_row, a_col, g_bf, g_col, constant
 
         def prepare_scores(h, jh):
-            s_row, t_col, floor_col, feat, feat_b = prepared[h]
+            feat, feat_b, c_row, a_col, g_bf, g_col = prepared[h][0:6]
             half = slice(jh * W, (jh + 1) * W)
             blocks = slice(jh * QB, (jh + 1) * QB)
             feat_ps = prep.tile([P, W], F32, tag="prep", name="feat_ps")
@@ -119,75 +128,95 @@ def tile_mgatlayer_b_kernel(tc, x, w, att_self, att_neigh, b, adj_t, base, offs,
                 nc.tensor.matmul(
                     t_ps[:, i : i + 1], feat[:, ub * P : (ub + 1) * P], att_cols[:, H + h : H + h + 1], start=True, stop=True
                 )
-            nc.scalar.mul(s_row[:, half], s_ps[:], 1.0 - SLOPE)
-            nc.scalar.copy(t_col[:, blocks], t_ps[:])
-            nc.scalar.activation(floor_col[:, blocks], t_ps[:], FN.Exp, scale=SLOPE)
+            nc.scalar.activation(c_row[:, half], s_ps[:], FN.Exp, scale=1.0 - SLOPE)
+            nc.scalar.activation(a_col[:, blocks], t_ps[:], FN.Exp, scale=1.0 - SLOPE)
+            nc.scalar.activation(g_bf[:, blocks], t_ps[:], FN.Exp, scale=SLOPE)
+            nc.scalar.copy(g_col[:, blocks], g_bf[:, blocks])
 
         def prepare_operand(h, jh):
-            feat_b = prepared[h][4]
-            blocks = slice(jh * QB, (jh + 1) * QB)
-            feat_t_ps = prep.tile([P, QB, P], BF16, tag="prep", name="feat_t_ps")
+            feat_b, g_col = prepared[h][1], prepared[h][5]
+            feat_t_ps = prep.tile([P, QB, P], F32, tag="prep", name="feat_t_ps")
             for i in range(QB):
                 ub = jh * QB + i
-                nc.tensor.transpose(feat_t_ps[:, i, :], feat_b[:, ub * P : (ub + 1) * P], ident_bf[:])
-            if h == 0:
-                nc.vector.tensor_copy(feat_b_t[h][:, blocks, :], feat_t_ps[:])
-            else:
-                nc.scalar.copy(feat_b_t[h][:, blocks, :], feat_t_ps[:])
+                nc.tensor.transpose(feat_t_ps[:, i, :], feat_b[:, ub * P : (ub + 1) * P], ident_f32[:])
+            for i in range(QB):
+                ub = jh * QB + i
+                if h == 0:
+                    nc.vector.tensor_scalar_mul(feat_b_g[h][:, ub, :], feat_t_ps[:, i, :], g_col[:, ub : ub + 1])
+                else:
+                    nc.scalar.mul(feat_b_g[h][:, ub, :], feat_t_ps[:, i, :], g_col[:, ub : ub + 1])
 
-        def exponential(k, ub):
-            s_row, t_col = prepared[k // JH][0:2]
+        def sum_operand(h):
+            constant_ps = prep.tile([P, 1], F32, tag="prep", name="constant_ps")
+            for ub in range(UB):
+                nc.tensor.matmul(
+                    constant_ps[:], feat_b_g[h][:, ub, :], ones[:, 0:1], start=(ub == 0), stop=(ub == UB - 1)
+                )
+            nc.scalar.copy(prepared[h][6][:], constant_ps[:])
+
+        def set_limit(i, jh):
+            part = adj[i][:, :, :, jh * W : (jh + 1) * W]
+            nc.vector.tensor_scalar(part, part, HUGE, -1.0, ALU.mult, ALU.add)
+
+        def relu_over(k, i):
+            c_row, a_col = prepared[k // JH][2:4]
             jh = k % JH
-            steep = ring.tile([P, W], BF16, name="steep", bufs=AHEAD + 2)
-            nc.scalar.activation(steep[:], s_row[:, jh * W : (jh + 1) * W], FN.Exp, bias=t_col[:, ub : ub + 1])
-            return steep
-
-        def maxima(k, i):
-            floor_col = prepared[k // JH][2]
-            e = ring.tile([P, PAIR, W], BF16, name="e")
+            over = ring.tile([P, PAIR, W], BF16, name="over", bufs=AHEAD + 1)
             for c in range(PAIR):
                 ub = i * PAIR + c
-                nc.vector.tensor_scalar_max(e[:, c, :], steep[k * UB + ub][:], floor_col[:, ub : ub + 1])
-            return e
+                nc.scalar.activation(
+                    over[:, c, :],
+                    c_row[:, jh * W : (jh + 1) * W],
+                    FN.Relu,
+                    bias=minus_one[:],
+                    scale=a_col[:, ub : ub + 1],
+                )
+            return over
 
-        def mask(k, i, e):
+        def mask(k, i, over):
             jh = k % JH
-            p = ring.tile([P, PAIR, R, W], BF16, name="p", bufs=2 * UB // PAIR)
+            q = ring.tile([P, PAIR, R, W], BF16, name="q", bufs=2 * PAIRS)
             nc.vector.tensor_tensor(
-                p[:], e[:].unsqueeze(2).to_broadcast([P, PAIR, R, W]), adj[i][:, :, :, jh * W : (jh + 1) * W], ALU.mult
+                q[:], over[:].unsqueeze(2).to_broadcast([P, PAIR, R, W]), adj[i][:, :, :, jh * W : (jh + 1) * W], ALU.min
             )
-            return p
+            return q
 
-        def add_block(k, ub, p, biased_ps):
+        def add_block(k, ub, q, biased_ps):
             for r in range(R):
                 nc.tensor.matmul(
                     biased_ps[r][:],
-                    feat_b_t[k // JH][:, ub, :],
-                    p[:, ub % PAIR, r, :],
+                    feat_b_g[k // JH][:, ub, :],
+                    q[:, ub % PAIR, r, :],
                     start=(ub == 0),
                     stop=(ub == UB - 1),
                 )
 
-        def sum_den(p_pairs):
-            den_ps = prep.tile([P, R, QB], F32, tag="prep", name="den_ps")
-            for r in range(R):
-                for q in range(QB):
-                    for ub in range(UB):
-                        nc.tensor.matmul(
-                            den_ps[:, r, q : q + 1],
-                            p_pairs[ub // PAIR][:, ub % PAIR, r, q * P : (q + 1) * P],
-                            ones[:, 0:1],
-                            start=(ub == 0),
-                            stop=(ub == UB - 1),
-                        )
+        def open_den(k):
+            g_bf = prepared[k // JH][4]
+            den_ps = prep.tile([P, R * QB], F32, tag="prep", name="den_ps")
+            for ub in range(UB):
+                nc.tensor.matmul(
+                    den_ps[:], ones[:], g_bf[:, ub : ub + 1].to_broadcast([P, R * QB]), start=(ub == 0), stop=False
+                )
             return den_ps
+
+        def add_den(k, ub, q, den_ps):
+            g_bf = prepared[k // JH][4]
+            for r in range(R):
+                for n in range(QB):
+                    nc.tensor.matmul(
+                        den_ps[:, r * QB + n : r * QB + n + 1],
+                        q[:, ub % PAIR, r, n * P : (n + 1) * P],
+                        g_bf[:, ub : ub + 1],
+                        start=False,
+                        stop=(ub == UB - 1 and r == R - 1 and n == QB - 1),
+                    )
 
         def spread_inverse(inv_cols, r):
             inv_ps = turn.tile([P, W], F32, name="inv_ps")
-            for q in range(QB):
-                nc.tensor.transpose(
-                    inv_ps[:, q * P : (q + 1) * P], inv_cols[:, r, q : q + 1].to_broadcast([P, P]), ident_f32[:]
-                )
+            for n in range(QB):
+                column = inv_cols[:, r * QB + n : r * QB + n + 1]
+                nc.tensor.transpose(inv_ps[:, n * P : (n + 1) * P], column.to_broadcast([P, P]), ident_f32[:])
             return inv_ps
 
         def scatter(k, r, positive, inv_den):
@@ -198,13 +227,14 @@ def tile_mgatlayer_b_kernel(tc, x, w, att_self, att_neigh, b, adj_t, base, offs,
                 row = r * M + h * P
                 nc.sync.dma_start(out[row : row + P, :], window[r, h][:])
 
-        BLOCKS = PASSES * UB
         prepared = {0: new_head()}
+        over = {}
         for jh in range(JH):
             prepare_scores(0, jh)
             prepare_operand(0, jh)
-        steep = {g: exponential(*divmod(g, UB)) for g in range(AHEAD)}
-        e_next = maxima(0, 0)
+            for n in range(jh * AHEAD // JH, (jh + 1) * AHEAD // JH):
+                over[n] = relu_over(*divmod(n, PAIRS))
+        sum_operand(0)
         positive, inv_ps, inv_den = {}, {}, {}
 
         def copy_inverse(k, r):
@@ -214,36 +244,42 @@ def tile_mgatlayer_b_kernel(tc, x, w, att_self, att_neigh, b, adj_t, base, offs,
         for k in range(PASSES + 1):
             if k < PASSES:
                 biased_ps = [acc.tile([P, W], F32, tag="acc", name=f"biased_ps{r}") for r in range(R)]
-                p_pairs = []
-                for i in range(UB // PAIR):
-                    for g in range(k * UB + i * PAIR, k * UB + (i + 1) * PAIR):
-                        if g + AHEAD < BLOCKS:
-                            if (g + AHEAD) % (JH * UB) == 0:
-                                prepared[(g + AHEAD) // (JH * UB)] = new_head()
-                                for jh in range(JH):
-                                    prepare_scores((g + AHEAD) // (JH * UB), jh)
-                            steep[g + AHEAD] = exponential(*divmod(g + AHEAD, UB))
-                            if (g + AHEAD) % (JH * UB) == 0:
-                                for jh in range(JH):
-                                    prepare_operand((g + AHEAD) // (JH * UB), jh)
-                    e = e_next
-                    if k * UB + (i + 1) * PAIR < BLOCKS:
-                        e_next = maxima(*divmod(k * (UB // PAIR) + i + 1, UB // PAIR))
-                    p_pairs.append(mask(k, i, e))
+                q_pairs = []
+                for i in range(PAIRS):
+                    n = k * PAIRS + i + AHEAD
+                    if n < PASSES * PAIRS:
+                        h = n // (JH * PAIRS)
+                        if n % (JH * PAIRS) == 0:
+                            prepared[h] = new_head()
+                            for jh in range(JH):
+                                prepare_scores(h, jh)
+                        over[n] = relu_over(*divmod(n, PAIRS))
+                        if n % (JH * PAIRS) == 0:
+                            for jh in range(JH):
+                                prepare_operand(h, jh)
+                            sum_operand(h)
+                    if k < JH:
+                        set_limit(i, k)
+                    q_pairs.append(mask(k, i, over[k * PAIRS + i]))
+                    if i == PAIRS - 1:
+                        den_ps = open_den(k)
+                        for ub in range(UB - PAIR):
+                            add_den(k, ub, q_pairs[ub // PAIR], den_ps)
                     for ub in range(i * PAIR, (i + 1) * PAIR):
-                        add_block(k, ub, p_pairs[i], biased_ps)
-                den_ps = sum_den(p_pairs)
+                        add_block(k, ub, q_pairs[i], biased_ps)
+                for ub in range(UB - PAIR, UB):
+                    add_den(k, ub, q_pairs[ub // PAIR], den_ps)
             if k > 0:
                 scatter(k - 1, 0, positive[k - 1, 0], inv_den[k - 1, 0])
             if k < PASSES:
                 for r in range(R):
                     positive[k, r] = ring.tile([P, W], F32, name=f"positive{r}")
-                    nc.scalar.activation(positive[k, r][:], biased_ps[r][:], FN.Relu)
-                inv_cols = ring.tile([P, R, QB], F32, name="inv_cols")
-                if k < PASSES - 1:
+                    nc.scalar.activation(positive[k, r][:], biased_ps[r][:], FN.Relu, bias=prepared[k // JH][6][:])
+                inv_cols = ring.tile([P, R * QB], F32, name="inv_cols")
+                if k < LAST_EXP:
                     nc.vector.reciprocal(inv_cols[:], den_ps[:])
                 else:
-                    inv_root = ring.tile([P, R, QB], F32, name="inv_root")
+                    inv_root = ring.tile([P, R * QB], F32, name="inv_root")
                     nc.scalar.activation(inv_root[:], den_ps[:], FN.Abs_reciprocal_sqrt)
                     nc.scalar.activation(inv_cols[:], inv_root[:], FN.Square)
                 inv_ps[k, 0] = spread_inverse(inv_cols, 0)

@@ -19,7 +19,6 @@ PASSES = H * JH
 PAIR = 2
 PAIRS = UB // PAIR
 AHEAD = PAIRS
-LAST_EXP = (H - 1) * JH - 1
 SLOPE = 0.2
 HUGE = 2.0**100
 
@@ -92,13 +91,13 @@ def tile_mgatlayer_b_kernel(tc, x, w, att_self, att_neigh, b, adj_t, base, offs,
         att_cols = held.tile([P, 2 * H], BF16, name="att_cols")
         nc.scalar.copy(att_cols[:], att_ps[:, 0 : 2 * H])
         att_self_rep = held.tile([P, H, P], BF16, name="att_self_rep")
-        nc.vector.tensor_copy(att_self_rep[:], att_cols[:, 0:H].unsqueeze(2).to_broadcast([P, H, P]))
+        nc.scalar.copy(att_self_rep[:], att_cols[:, 0:H].unsqueeze(2).to_broadcast([P, H, P]))
 
         feat_b_g = [held.tile([P, UB, P], BF16, name=f"feat_b_g{h}") for h in range(H)]
 
         def new_head():
             feat = head.tile([P, N], BF16, name="feat")
-            feat_b = head.tile([P, N], F32, name="feat_b")
+            feat_b = head.tile([P, N], BF16, name="feat_b")
             c_row = head.tile([P, N], F32, name="c_row")
             a_col = head.tile([P, UB], F32, name="a_col")
             g_bf = head.tile([P, UB], BF16, name="g_bf")
@@ -107,7 +106,8 @@ def tile_mgatlayer_b_kernel(tc, x, w, att_self, att_neigh, b, adj_t, base, offs,
             return feat, feat_b, c_row, a_col, g_bf, g_col, constant
 
         def prepare_scores(h, jh):
-            feat, feat_b, c_row, a_col, g_bf, g_col = prepared[h][0:6]
+            feat, feat_b = prepared[h][0:2]
+            a_col, g_bf, g_col = prepared[h][3:6]
             half = slice(jh * W, (jh + 1) * W)
             blocks = slice(jh * QB, (jh + 1) * QB)
             feat_ps = prep.tile([P, W], F32, tag="prep", name="feat_ps")
@@ -120,25 +120,29 @@ def tile_mgatlayer_b_kernel(tc, x, w, att_self, att_neigh, b, adj_t, base, offs,
                 nc.vector.tensor_scalar_add(feat_b[:, half], feat_ps[:], b_cols[:, h : h + 1])
             else:
                 nc.scalar.activation(feat_b[:, half], feat_ps[:], FN.Identity, bias=b_cols[:, h : h + 1])
-            s_ps = prep.tile([P, W], F32, tag="prep", name="s_ps")
-            nc.tensor.matmul(s_ps[:], att_self_rep[:, h, :], feat[:, half], start=True, stop=True)
             t_ps = prep.tile([P, QB], F32, tag="prep", name="t_ps")
             for i in range(QB):
                 ub = jh * QB + i
                 nc.tensor.matmul(
                     t_ps[:, i : i + 1], feat[:, ub * P : (ub + 1) * P], att_cols[:, H + h : H + h + 1], start=True, stop=True
                 )
-            nc.scalar.activation(c_row[:, half], s_ps[:], FN.Exp, scale=1.0 - SLOPE)
             nc.scalar.activation(a_col[:, blocks], t_ps[:], FN.Exp, scale=1.0 - SLOPE)
             nc.scalar.activation(g_bf[:, blocks], t_ps[:], FN.Exp, scale=SLOPE)
             nc.scalar.copy(g_col[:, blocks], g_bf[:, blocks])
 
+        def prepare_row(h, jh):
+            feat, c_row = prepared[h][0], prepared[h][2]
+            half = slice(jh * W, (jh + 1) * W)
+            s_ps = prep.tile([P, W], F32, tag="prep", name="s_ps")
+            nc.tensor.matmul(s_ps[:], att_self_rep[:, h, :], feat[:, half], start=True, stop=True)
+            nc.scalar.activation(c_row[:, half], s_ps[:], FN.Exp, scale=1.0 - SLOPE)
+
         def prepare_operand(h, jh):
             feat_b, g_col = prepared[h][1], prepared[h][5]
-            feat_t_ps = prep.tile([P, QB, P], F32, tag="prep", name="feat_t_ps")
+            feat_t_ps = prep.tile([P, QB, P], BF16, tag="prep", name="feat_t_ps")
             for i in range(QB):
                 ub = jh * QB + i
-                nc.tensor.transpose(feat_t_ps[:, i, :], feat_b[:, ub * P : (ub + 1) * P], ident_f32[:])
+                nc.tensor.transpose(feat_t_ps[:, i, :], feat_b[:, ub * P : (ub + 1) * P], ident_bf[:])
             for i in range(QB):
                 ub = jh * QB + i
                 if h == 0:
@@ -154,9 +158,11 @@ def tile_mgatlayer_b_kernel(tc, x, w, att_self, att_neigh, b, adj_t, base, offs,
                 )
             nc.scalar.copy(prepared[h][6][:], constant_ps[:])
 
+        huge = held.tile([P, 1], F32, name="huge")
+
         def set_limit(i, jh):
             part = adj[i][:, :, :, jh * W : (jh + 1) * W]
-            nc.vector.tensor_scalar(part, part, HUGE, -1.0, ALU.mult, ALU.add)
+            nc.vector.tensor_scalar(part, part, huge[:], -1.0, ALU.mult, ALU.add)
 
         def relu_over(k, i):
             c_row, a_col = prepared[k // JH][2:4]
@@ -228,12 +234,17 @@ def tile_mgatlayer_b_kernel(tc, x, w, att_self, att_neigh, b, adj_t, base, offs,
                 nc.sync.dma_start(out[row : row + P, :], window[r, h][:])
 
         prepared = {0: new_head()}
-        over = {}
-        for jh in range(JH):
-            prepare_scores(0, jh)
-            prepare_operand(0, jh)
-            for n in range(jh * AHEAD // JH, (jh + 1) * AHEAD // JH):
-                over[n] = relu_over(*divmod(n, PAIRS))
+        prepare_scores(0, 0)
+        nc.vector.tensor_scalar(huge[:], prepared[0][0][:, 0:1], 0.0, HUGE, ALU.mult, ALU.add)
+        prepare_row(0, 0)
+        prepare_operand(0, 0)
+        over = {0: relu_over(0, 0)}
+        prepare_scores(0, 1)
+        over[1] = relu_over(0, 1)
+        prepare_operand(0, 1)
+        for n in range(PAIRS // 2, PAIRS):
+            over[n] = relu_over(0, n)
+        prepare_row(0, 1)
         sum_operand(0)
         positive, inv_ps, inv_den = {}, {}, {}
 
@@ -253,6 +264,7 @@ def tile_mgatlayer_b_kernel(tc, x, w, att_self, att_neigh, b, adj_t, base, offs,
                             prepared[h] = new_head()
                             for jh in range(JH):
                                 prepare_scores(h, jh)
+                                prepare_row(h, jh)
                         over[n] = relu_over(*divmod(n, PAIRS))
                         if n % (JH * PAIRS) == 0:
                             for jh in range(JH):
@@ -276,7 +288,7 @@ def tile_mgatlayer_b_kernel(tc, x, w, att_self, att_neigh, b, adj_t, base, offs,
                     positive[k, r] = ring.tile([P, W], F32, name=f"positive{r}")
                     nc.scalar.activation(positive[k, r][:], biased_ps[r][:], FN.Relu, bias=prepared[k // JH][6][:])
                 inv_cols = ring.tile([P, R * QB], F32, name="inv_cols")
-                if k < LAST_EXP:
+                if k < PASSES - 2:
                     nc.vector.reciprocal(inv_cols[:], den_ps[:])
                 else:
                     inv_root = ring.tile([P, R * QB], F32, name="inv_root")

@@ -116,7 +116,7 @@ def tile_mgatlayer_b_kernel(tc, x, w, att_self, att_neigh, b, adj_t, base, offs,
                     feat_ps[:], w_sb[:, k, h * P : (h + 1) * P], x_sb[:, k, half], start=(k == 0), stop=(k == FB - 1)
                 )
             nc.scalar.copy(feat[:, half], feat_ps[:])
-            if h == 0:
+            if h == 0 and jh == 0:
                 nc.vector.tensor_scalar_add(feat_b[:, half], feat_ps[:], b_cols[:, h : h + 1])
             else:
                 nc.scalar.activation(feat_b[:, half], feat_ps[:], FN.Identity, bias=b_cols[:, h : h + 1])
@@ -128,7 +128,10 @@ def tile_mgatlayer_b_kernel(tc, x, w, att_self, att_neigh, b, adj_t, base, offs,
                 )
             nc.scalar.activation(a_col[:, blocks], t_ps[:], FN.Exp, scale=1.0 - SLOPE)
             nc.scalar.activation(g_bf[:, blocks], t_ps[:], FN.Exp, scale=SLOPE)
-            nc.scalar.copy(g_col[:, blocks], g_bf[:, blocks])
+            if h == 0:
+                nc.vector.tensor_copy(g_col[:, blocks], g_bf[:, blocks])
+            else:
+                nc.scalar.copy(g_col[:, blocks], g_bf[:, blocks])
 
         def prepare_row(h, jh):
             feat, c_row = prepared[h][0], prepared[h][2]
@@ -158,10 +161,12 @@ def tile_mgatlayer_b_kernel(tc, x, w, att_self, att_neigh, b, adj_t, base, offs,
                 )
             nc.scalar.copy(prepared[h][6][:], constant_ps[:])
 
-        huge = held.tile([P, 1], F32, name="huge")
+        huge_first = held.tile([P, 1], F32, name="huge_first")
+        huge_later = held.tile([P, 1], F32, name="huge_later")
 
         def set_limit(i, jh):
             part = adj[i][:, :, :, jh * W : (jh + 1) * W]
+            huge = huge_first if jh == 0 and i < 2 else huge_later
             nc.vector.tensor_scalar(part, part, huge[:], -1.0, ALU.mult, ALU.add)
 
         def relu_over(k, i):
@@ -235,10 +240,11 @@ def tile_mgatlayer_b_kernel(tc, x, w, att_self, att_neigh, b, adj_t, base, offs,
 
         prepared = {0: new_head()}
         prepare_scores(0, 0)
-        nc.vector.tensor_scalar(huge[:], prepared[0][0][:, 0:1], 0.0, HUGE, ALU.mult, ALU.add)
+        nc.vector.tensor_scalar(huge_first[:], prepared[0][0][:, 0:1], 0.0, HUGE, ALU.mult, ALU.add)
         prepare_row(0, 0)
         prepare_operand(0, 0)
         over = {0: relu_over(0, 0)}
+        nc.vector.tensor_scalar(huge_later[:], over[0][:, 0, 0:1], 0.0, HUGE, ALU.mult, ALU.add)
         prepare_scores(0, 1)
         over[1] = relu_over(0, 1)
         prepare_operand(0, 1)

@@ -39,6 +39,9 @@ def tile_mgatlayer_b_kernel(tc, x, w, att_self, att_neigh, b, adj_t, base, offs,
         nc.vector.memset(att_rows[:], 0.0)
         nc.sync.dma_start(att_rows[0:H, :], att_self.rearrange("(h d) o -> h (d o)", d=P))
         nc.sync.dma_start(att_rows[H : 2 * H, :], att_neigh.rearrange("(h d) o -> h (d o)", d=P))
+        b_rows = held.tile([P, P], F32, name="b_rows")
+        nc.gpsimd.memset(b_rows[:], 0.0)
+        nc.sync.dma_start(b_rows[0:H, :], b.rearrange("(h d) o -> h (d o)", d=P))
         w_sb = held.tile([P, FB, M], BF16, name="w_sb")
         x_sb = held.tile([P, FB, N], BF16, name="x_sb")
         adj = [held.tile([P, PAIR, R, N], BF16, name=f"adj{i}") for i in range(UB // PAIR)]
@@ -56,8 +59,6 @@ def tile_mgatlayer_b_kernel(tc, x, w, att_self, att_neigh, b, adj_t, base, offs,
 
         nc.sync.dma_start(w_sb[:, :, 0:P], w_blocks[:, :, 0:P])
         load_x(0)
-        b_cols = held.tile([P, H], F32, name="b_cols")
-        nc.sync.dma_start(b_cols[:], b.rearrange("(h d) o -> d (h o)", d=P))
         for ub in range(PAIR):
             load_adj(ub, 0)
         load_x(1)
@@ -90,6 +91,10 @@ def tile_mgatlayer_b_kernel(tc, x, w, att_self, att_neigh, b, adj_t, base, offs,
         nc.tensor.transpose(att_ps[:], att_rows[:], ident_bf[:])
         att_cols = held.tile([P, 2 * H], BF16, name="att_cols")
         nc.scalar.copy(att_cols[:], att_ps[:, 0 : 2 * H])
+        b_ps = prep.tile([P, P], F32, tag="prep", name="b_ps")
+        nc.tensor.transpose(b_ps[:], b_rows[:], ident_f32[:])
+        b_cols = held.tile([P, H], F32, name="b_cols")
+        nc.scalar.copy(b_cols[:], b_ps[:, 0:H])
         att_self_rep = held.tile([P, H, P], BF16, name="att_self_rep")
         nc.scalar.copy(att_self_rep[:], att_cols[:, 0:H].unsqueeze(2).to_broadcast([P, H, P]))
 
@@ -244,7 +249,7 @@ def tile_mgatlayer_b_kernel(tc, x, w, att_self, att_neigh, b, adj_t, base, offs,
         prepare_row(0, 0)
         prepare_operand(0, 0)
         over = {0: relu_over(0, 0)}
-        nc.vector.tensor_scalar(huge_later[:], over[0][:, 0, 0:1], 0.0, HUGE, ALU.mult, ALU.add)
+        nc.vector.tensor_scalar(huge_later[:], over[0][:, PAIR - 1, 0:1], 0.0, HUGE, ALU.mult, ALU.add)
         prepare_scores(0, 1)
         over[1] = relu_over(0, 1)
         prepare_operand(0, 1)

@@ -64,9 +64,9 @@ def tile_mgatlayer_b_kernel(tc, x, w, att_self, att_neigh, b, adj_t, base, offs,
         load_x(1)
         for ub in range(PAIR, UB // 2):
             load_adj(ub, 0)
-        nc.sync.dma_start(w_sb[:, :, P:M], w_blocks[:, :, P:M])
         for ub in range(UB // 2, UB):
             load_adj(ub, 0)
+        nc.sync.dma_start(w_sb[:, :, P:M], w_blocks[:, :, P:M])
         offsets = held.tile([P, N // 16], U16, name="offsets")
         nc.sync.dma_start(offsets[:], offs)
         for ub in range(UB):
@@ -241,7 +241,11 @@ def tile_mgatlayer_b_kernel(tc, x, w, att_self, att_neigh, b, adj_t, base, offs,
             nc.vector.tensor_tensor(window[r, h][:].indirect(piece), positive[:], inv_den[:], ALU.mult)
             if jh == JH - 1:
                 row = r * M + h * P
-                nc.sync.dma_start(out[row : row + P, :], window[r, h][:])
+                if (h, r) == (H - 1, R - 1):
+                    nc.scalar.dma_start(out[row : row + P, 0 : S // 2], window[r, h][:, 0 : S // 2])
+                    nc.sync.dma_start(out[row : row + P, S // 2 : S], window[r, h][:, S // 2 : S])
+                else:
+                    nc.sync.dma_start(out[row : row + P, :], window[r, h][:])
 
         prepared = {0: new_head()}
         prepare_scores(0, 0)

from contextlib import ExitStack

import concourse.mybir as mybir
from concourse.masks import make_identity

F32, BF16, U16 = mybir.dt.float32, mybir.dt.bfloat16, mybir.dt.uint16
FN = mybir.ActivationFunctionType
ALU = mybir.AluOpType

P = 128
F, H, R, N, S = 512, 4, 2, 1024, 2048
M = H * P
FB = F // P
UB = N // P
W = 512
JH = N // W
QB = W // P
PASSES = H * JH
PAIR = 2
PAIRS = UB // PAIR
AHEAD = PAIRS
SLOPE = 0.2
HUGE = 2.0**100

FLOPS = 2 * F * M * N + 4 * M * N + 2 * R * M * N * N + 2 * R * H * N * N


def tile_mgatlayer_b_kernel(tc, x, w, att_self, att_neigh, b, adj_t, base, offs, out):
    nc = tc.nc
    with ExitStack() as ctx:
        held = ctx.enter_context(tc.tile_pool(name="held", bufs=1))
        head = ctx.enter_context(tc.tile_pool(name="head", bufs=2))
        ring = ctx.enter_context(tc.tile_pool(name="ring", bufs=4))
        prep = ctx.enter_context(tc.psum_pool(name="prep", bufs=4))
        acc = ctx.enter_context(tc.psum_pool(name="acc", bufs=R))
        turn = ctx.enter_context(tc.psum_pool(name="turn", bufs=R))

        att_rows = held.tile([P, P], BF16, name="att_rows")
        nc.vector.memset(att_rows[:], 0.0)
        nc.sync.dma_start(att_rows[0:H, :], att_self.rearrange("(h d) o -> h (d o)", d=P))
        nc.sync.dma_start(att_rows[H : 2 * H, :], att_neigh.rearrange("(h d) o -> h (d o)", d=P))
        b_rows = held.tile([P, P], F32, name="b_rows")
        nc.gpsimd.memset(b_rows[:], 0.0)
        nc.sync.dma_start(b_rows[0:H, :], b.rearrange("(h d) o -> h (d o)", d=P))
        w_sb = held.tile([P, FB, M], BF16, name="w_sb")
        x_sb = held.tile([P, FB, N], BF16, name="x_sb")
        adj = [held.tile([P, PAIR, R, N], BF16, name=f"adj{i}") for i in range(UB // PAIR)]
        w_blocks = w.rearrange("(k p) m -> p k m", p=P)

        def load_x(jh):
            for k in range(FB):
                nc.sync.dma_start(x_sb[:, k, jh * W : (jh + 1) * W], x[k * P : (k + 1) * P, jh * W : (jh + 1) * W])

        def load_adj(ub, jh):
            nc.sync.dma_start(
                adj[ub // PAIR][:, ub % PAIR, :, jh * W : (jh + 1) * W],
                adj_t[:, ub * P : (ub + 1) * P, jh * W : (jh + 1) * W].rearrange("r u j -> u r j"),
            )

        nc.sync.dma_start(w_sb[:, :, 0:P], w_blocks[:, :, 0:P])
        load_x(0)
        for ub in range(PAIR):
            load_adj(ub, 0)
        load_x(1)
        for ub in range(PAIR, UB // 2):
            load_adj(ub, 0)
        for ub in range(UB // 2, UB):
            load_adj(ub, 0)
        nc.sync.dma_start(w_sb[:, :, P:M], w_blocks[:, :, P:M])
        offsets = held.tile([P, N // 16], U16, name="offsets")
        nc.sync.dma_start(offsets[:], offs)
        for ub in range(UB):
            load_adj(ub, 1)
        window = {}
        for h in range(H):
            for r in range(R):
                window[r, h] = held.tile([P, S], F32, name=f"window{r}{h}")
                row = r * M + h * P
                nc.sync.dma_start(window[r, h][:], base[row : row + P, :])

        ident_bf = held.tile([P, P], BF16, name="ident_bf")
        ident_f32 = held.tile([P, P], F32, name="ident_f32")
        make_identity(nc, ident_bf[:])
        make_identity(nc, ident_f32[:])
        ones = held.tile([P, P], BF16, name="ones")
        nc.gpsimd.memset(ones[:], 1.0)
        minus_one = held.tile([P, 1], F32, name="minus_one")
        nc.gpsimd.memset(minus_one[:], -1.0)

        att_ps = prep.tile([P, P], BF16, tag="prep", name="att_ps")
        nc.tensor.transpose(att_ps[:], att_rows[:], ident_bf[:])
        att_cols = held.tile([P, 2 * H], BF16, name="att_cols")
        nc.scalar.copy(att_cols[:], att_ps[:, 0 : 2 * H])
        b_ps = prep.tile([P, P], F32, tag="prep", name="b_ps")
        nc.tensor.transpose(b_ps[:], b_rows[:], ident_f32[:])
        b_cols = held.tile([P, H], F32, name="b_cols")
        nc.scalar.copy(b_cols[:], b_ps[:, 0:H])
        att_self_rep = held.tile([P, H, P], BF16, name="att_self_rep")
        nc.scalar.copy(att_self_rep[:], att_cols[:, 0:H].unsqueeze(2).to_broadcast([P, H, P]))

        feat_b_g = [held.tile([P, UB, P], BF16, name=f"feat_b_g{h}") for h in range(H)]

        def new_head():
            feat = head.tile([P, N], BF16, name="feat")
            feat_b = head.tile([P, N], BF16, name="feat_b")
            c_row = head.tile([P, N], F32, name="c_row")
            a_col = head.tile([P, UB], F32, name="a_col")
            g_bf = head.tile([P, UB], BF16, name="g_bf")
            g_col = head.tile([P, UB], F32, name="g_col")
            constant = head.tile([P, 1], F32, name="constant")
            return feat, feat_b, c_row, a_col, g_bf, g_col, constant

        def prepare_scores(h, jh):
            feat, feat_b = prepared[h][0:2]
            a_col, g_bf, g_col = prepared[h][3:6]
            half = slice(jh * W, (jh + 1) * W)
            blocks = slice(jh * QB, (jh + 1) * QB)
            feat_ps = prep.tile([P, W], F32, tag="prep", name="feat_ps")
            for k in range(FB):
                nc.tensor.matmul(
                    feat_ps[:], w_sb[:, k, h * P : (h + 1) * P], x_sb[:, k, half], start=(k == 0), stop=(k == FB - 1)
                )
            nc.scalar.copy(feat[:, half], feat_ps[:])
            if h == 0 and jh == 0:
                nc.vector.tensor_scalar_add(feat_b[:, half], feat_ps[:], b_cols[:, h : h + 1])
            else:
                nc.scalar.activation(feat_b[:, half], feat_ps[:], FN.Identity, bias=b_cols[:, h : h + 1])
            t_ps = prep.tile([P, QB], F32, tag="prep", name="t_ps")
            for i in range(QB):
                ub = jh * QB + i
                nc.tensor.matmul(
                    t_ps[:, i : i + 1], feat[:, ub * P : (ub + 1) * P], att_cols[:, H + h : H + h + 1], start=True, stop=True
                )
            nc.scalar.activation(a_col[:, blocks], t_ps[:], FN.Exp, scale=1.0 - SLOPE)
            nc.scalar.activation(g_bf[:, blocks], t_ps[:], FN.Exp, scale=SLOPE)
            if h == 0:
                nc.vector.tensor_copy(g_col[:, blocks], g_bf[:, blocks])
            else:
                nc.scalar.copy(g_col[:, blocks], g_bf[:, blocks])

        def prepare_row(h, jh):
            feat, c_row = prepared[h][0], prepared[h][2]
            half = slice(jh * W, (jh + 1) * W)
            s_ps = prep.tile([P, W], F32, tag="prep", name="s_ps")
            nc.tensor.matmul(s_ps[:], att_self_rep[:, h, :], feat[:, half], start=True, stop=True)
            nc.scalar.activation(c_row[:, half], s_ps[:], FN.Exp, scale=1.0 - SLOPE)

        def prepare_operand(h, jh):
            feat_b, g_col = prepared[h][1], prepared[h][5]
            feat_t_ps = prep.tile([P, QB, P], BF16, tag="prep", name="feat_t_ps")
            for i in range(QB):
                ub = jh * QB + i
                nc.tensor.transpose(feat_t_ps[:, i, :], feat_b[:, ub * P : (ub + 1) * P], ident_bf[:])
            for i in range(QB):
                ub = jh * QB + i
                if h == 0:
                    nc.vector.tensor_scalar_mul(feat_b_g[h][:, ub, :], feat_t_ps[:, i, :], g_col[:, ub : ub + 1])
                else:
                    nc.scalar.mul(feat_b_g[h][:, ub, :], feat_t_ps[:, i, :], g_col[:, ub : ub + 1])

        def sum_operand(h):
            constant_ps = prep.tile([P, 1], F32, tag="prep", name="constant_ps")
            for ub in range(UB):
                nc.tensor.matmul(
                    constant_ps[:], feat_b_g[h][:, ub, :], ones[:, 0:1], start=(ub == 0), stop=(ub == UB - 1)
                )
            nc.scalar.copy(prepared[h][6][:], constant_ps[:])

        huge_first = held.tile([P, 1], F32, name="huge_first")
        huge_later = held.tile([P, 1], F32, name="huge_later")

        def set_limit(i, jh):
            part = adj[i][:, :, :, jh * W : (jh + 1) * W]
            huge = huge_first if jh == 0 and i < 2 else huge_later
            nc.vector.tensor_scalar(part, part, huge[:], -1.0, ALU.mult, ALU.add)

        def relu_over(k, i):
            c_row, a_col = prepared[k // JH][2:4]
            jh = k % JH
            over = ring.tile([P, PAIR, W], BF16, name="over", bufs=AHEAD + 1)
            for c in range(PAIR):
                ub = i * PAIR + c
                nc.scalar.activation(
                    over[:, c, :],
                    c_row[:, jh * W : (jh + 1) * W],
                    FN.Relu,
                    bias=minus_one[:],
                    scale=a_col[:, ub : ub + 1],
                )
            return over

        def mask(k, i, over):
            jh = k % JH
            q = ring.tile([P, PAIR, R, W], BF16, name="q", bufs=2 * PAIRS)
            nc.vector.tensor_tensor(
                q[:], over[:].unsqueeze(2).to_broadcast([P, PAIR, R, W]), adj[i][:, :, :, jh * W : (jh + 1) * W], ALU.min
            )
            return q

        def add_block(k, ub, q, biased_ps):
            for r in range(R):
                nc.tensor.matmul(
                    biased_ps[r][:],
                    feat_b_g[k // JH][:, ub, :],
                    q[:, ub % PAIR, r, :],
                    start=(ub == 0),
                    stop=(ub == UB - 1),
                )

        def open_den(k):
            g_bf = prepared[k // JH][4]
            den_ps = prep.tile([P, R * QB], F32, tag="prep", name="den_ps")
            for ub in range(UB):
                nc.tensor.matmul(
                    den_ps[:], ones[:], g_bf[:, ub : ub + 1].to_broadcast([P, R * QB]), start=(ub == 0), stop=False
                )
            return den_ps

        def add_den(k, ub, q, den_ps):
            g_bf = prepared[k // JH][4]
            for r in range(R):
                for n in range(QB):
                    nc.tensor.matmul(
                        den_ps[:, r * QB + n : r * QB + n + 1],
                        q[:, ub % PAIR, r, n * P : (n + 1) * P],
                        g_bf[:, ub : ub + 1],
                        start=False,
                        stop=(ub == UB - 1 and r == R - 1 and n == QB - 1),
                    )

        def spread_inverse(inv_cols, r):
            inv_ps = turn.tile([P, W], F32, name="inv_ps")
            for n in range(QB):
                column = inv_cols[:, r * QB + n : r * QB + n + 1]
                nc.tensor.transpose(inv_ps[:, n * P : (n + 1) * P], column.to_broadcast([P, P]), ident_f32[:])
            return inv_ps

        def scatter(k, r, positive, inv_den):
            h, jh = divmod(k, JH)
            piece = offsets[:, jh * (W // 16) : (jh + 1) * (W // 16)]
            nc.vector.tensor_tensor(window[r, h][:].indirect(piece), positive[:], inv_den[:], ALU.mult)
            if jh == JH - 1:
                row = r * M + h * P
                if (h, r) == (H - 1, R - 1):
                    nc.scalar.dma_start(out[row : row + P, 0 : S // 2], window[r, h][:, 0 : S // 2])
                    nc.sync.dma_start(out[row : row + P, S // 2 : S], window[r, h][:, S // 2 : S])
                else:
                    nc.sync.dma_start(out[row : row + P, :], window[r, h][:])

        prepared = {0: new_head()}
        prepare_scores(0, 0)
        nc.vector.tensor_scalar(huge_first[:], prepared[0][0][:, 0:1], 0.0, HUGE, ALU.mult, ALU.add)
        prepare_row(0, 0)
        prepare_operand(0, 0)
        over = {0: relu_over(0, 0)}
        nc.vector.tensor_scalar(huge_later[:], over[0][:, PAIR - 1, 0:1], 0.0, HUGE, ALU.mult, ALU.add)
        prepare_scores(0, 1)
        over[1] = relu_over(0, 1)
        prepare_operand(0, 1)
        for n in range(PAIRS // 2, PAIRS):
            over[n] = relu_over(0, n)
        prepare_row(0, 1)
        sum_operand(0)
        positive, inv_ps, inv_den = {}, {}, {}

        def copy_inverse(k, r):
            inv_den[k, r] = ring.tile([P, W], F32, name=f"inv_den{r}")
            nc.scalar.copy(inv_den[k, r][:], inv_ps[k, r][:])

        for k in range(PASSES + 1):
            if k < PASSES:
                biased_ps = [acc.tile([P, W], F32, tag="acc", name=f"biased_ps{r}") for r in range(R)]
                q_pairs = []
                for i in range(PAIRS):
                    n = k * PAIRS + i + AHEAD
                    if n < PASSES * PAIRS:
                        h = n // (JH * PAIRS)
                        if n % (JH * PAIRS) == 0:
                            prepared[h] = new_head()
                            for jh in range(JH):
                                prepare_scores(h, jh)
                                prepare_row(h, jh)
                        over[n] = relu_over(*divmod(n, PAIRS))
                        if n % (JH * PAIRS) == 0:
                            for jh in range(JH):
                                prepare_operand(h, jh)
                            sum_operand(h)
                    if k < JH:
                        set_limit(i, k)
                    q_pairs.append(mask(k, i, over[k * PAIRS + i]))
                    if i == PAIRS - 1:
                        den_ps = open_den(k)
                        for ub in range(UB - PAIR):
                            add_den(k, ub, q_pairs[ub // PAIR], den_ps)
                    for ub in range(i * PAIR, (i + 1) * PAIR):
                        add_block(k, ub, q_pairs[i], biased_ps)
                for ub in range(UB - PAIR, UB):
                    add_den(k, ub, q_pairs[ub // PAIR], den_ps)
            if k > 0:
                scatter(k - 1, 0, positive[k - 1, 0], inv_den[k - 1, 0])
            if k < PASSES:
                for r in range(R):
                    positive[k, r] = ring.tile([P, W], F32, name=f"positive{r}")
                    nc.scalar.activation(positive[k, r][:], biased_ps[r][:], FN.Relu, bias=prepared[k // JH][6][:])
                inv_cols = ring.tile([P, R * QB], F32, name="inv_cols")
                if k < PASSES - 2:
                    nc.vector.reciprocal(inv_cols[:], den_ps[:])
                else:
                    inv_root = ring.tile([P, R * QB], F32, name="inv_root")
                    nc.scalar.activation(inv_root[:], den_ps[:], FN.Abs_reciprocal_sqrt)
                    nc.scalar.activation(inv_cols[:], inv_root[:], FN.Square)
                inv_ps[k, 0] = spread_inverse(inv_cols, 0)
            if k > 0:
                copy_inverse(k - 1, 1)
            if k < PASSES:
                inv_ps[k, 1] = spread_inverse(inv_cols, 1)
            if k > 0:
                scatter(k - 1, 1, positive[k - 1, 1], inv_den[k - 1, 1])
            if k < PASSES:
                copy_inverse(k, 0)
